import numpy as np
import ml_dtypes


def mxq(x, axis, fmt="e4m3"):
    dtype, down = {"e4m3": (ml_dtypes.float8_e4m3fn, 7), "e5m2": (ml_dtypes.float8_e5m2, 14)}[fmt]
    v = np.moveaxis(np.asarray(x, np.float32).astype(ml_dtypes.bfloat16).astype(np.float64), axis, -1)
    blocks = v.reshape(v.shape[:-1] + (-1, 32))
    amax = np.abs(blocks).max(-1, keepdims=True)
    byte = np.maximum(np.where(amax > 0, np.frexp(amax)[1] - 1 + 127, 0) - down, 1)
    scale = np.exp2(byte - 127.0)
    codes = (blocks / scale).astype(np.float32).astype(dtype).astype(np.float64)
    return np.moveaxis((codes * scale).reshape(v.shape), -1, axis)


WIDE = False


def mx_kscale(k):
    if not WIDE:
        return np.ones(k)
    levels = np.array([10, -10, 5, -5, 0])
    if k % 512:
        return np.exp2(np.random.permutation(np.resize(levels, k // 32))).repeat(32)
    a = np.empty((k // 512, 16))
    for p in range(k // 512):
        a[p, :8] = np.random.permutation(np.resize(levels, 8))
        for g in range(8):
            far = levels[np.abs(levels - a[p, g]) >= 10]
            a[p, g + 8] = far[np.random.randint(len(far))]
    return np.exp2(a.ravel()).repeat(32)


BF16 = ml_dtypes.bfloat16


def bf(x):
    return np.asarray(x, np.float32).astype(BF16)


def f64(x):
    return np.asarray(x).astype(np.float64)


E2M1 = np.array([0.0, 0.5, 1.0, 1.5, 2.0, 3.0, 4.0, 6.0, -0.0, -0.5, -1.0, -1.5, -2.0, -3.0, -4.0, -6.0])


def pack_weight(w, fmt):
    k, n = w.shape
    w = f64(bf(w)).reshape(k // 32, 32, n)
    amax = np.abs(w).max(1)
    if fmt == "e4m3":
        byte = np.frexp(amax)[1] - 1 + 127 - 7
    else:
        mant, ex = np.frexp(amax / 6.0)
        byte = np.where(mant > 0.5, ex, ex - 1) + 127
    byte = np.clip(np.where(amax > 0, byte, 1), 1, 254)
    scaled = (w * np.exp2(127.0 - byte)[:, None, :]).reshape(k, n).astype(np.float32)
    by_word = np.ascontiguousarray(scaled.reshape(k // 512, 128, 4, n).transpose(0, 1, 3, 2))
    if fmt == "e4m3":
        words = by_word.astype(ml_dtypes.float8_e4m3fn).view(np.uint8)
    else:
        c = by_word.astype(ml_dtypes.float4_e2m1fn).view(np.uint8) & 0xF
        words = c[..., 0::2] | (c[..., 1::2] << 4)
    return np.ascontiguousarray(words), np.ascontiguousarray(byte.astype(np.uint8).reshape(k // 512, 16, n))


def unpack_weight(words, scales, fmt):
    g, p, n, _ = words.shape
    if fmt == "e4m3":
        vals = np.ascontiguousarray(words).view(ml_dtypes.float8_e4m3fn).astype(np.float64)
    else:
        nib = np.empty((g, p, n, 4), np.uint8)
        nib[..., 0::2] = words & 0xF
        nib[..., 1::2] = words >> 4
        vals = E2M1[nib]
    vals = vals * np.repeat(np.exp2(scales.astype(np.float64) - 127.0), 8, axis=1)[..., None]
    return vals.transpose(0, 1, 3, 2).reshape(g * 512, n)
def pack4(w):
    words, scales = pack_weight(w, "e2m1")
    return words.reshape(words.shape[0], 128, -1), scales


def unpack4(words, scales):
    return unpack_weight(words.reshape(words.shape[0], 128, -1, 2), scales, "e2m1")


B, T, C_IN, HIDDEN, HEADS, OUT_DIM = 4, 2048, 512, 512, 8, 512
RMS_EPS = 1.1920928955078125e-07


def silu(z):
    return z / (1.0 + np.exp(-z))


def draw0():
    s, t = mx_kscale(C_IN), mx_kscale(HIDDEN)
    r = np.exp2(-12.0 * np.random.random((B, T, 1)))
    x = bf(np.random.standard_normal((B, T, C_IN)) * s)
    h_attn = bf(np.random.standard_normal((B, T, HIDDEN)) * 0.8 * r)
    Wu_words, Wu_scales = pack4((np.random.standard_normal((HIDDEN, C_IN)) / np.sqrt(C_IN) / s).T)
    bu = bf(np.random.standard_normal(HIDDEN) * 0.1)
    g_norm = bf((1.0 + 0.1 * np.random.standard_normal(HIDDEN)) * t)
    Wf_words, Wf_scales = pack4((np.random.standard_normal((OUT_DIM, HIDDEN)) / np.sqrt(HIDDEN) / t).T)
    b_out = bf(np.random.standard_normal(OUT_DIM) * 0.1)
    return {"x": x,
            "h_attn": h_attn,
            "Wu_words": Wu_words,
            "Wu_scales": Wu_scales,
            "bu": bu,
            "g_norm": g_norm,
            "Wf_words": Wf_words,
            "Wf_scales": Wf_scales,
            "b_out": b_out}


def core(x, h_attn, Wu_words, Wu_scales, bu, g_norm, Wf_words, Wf_scales, b_out):
    u = silu((mxq(f64(x), 2, "e4m3") @ unpack4(Wu_words, Wu_scales)) + f64(bu))
    av = f64(h_attn)
    av_norm = av * (1.0 / np.sqrt(np.mean(av * av, axis=-1, keepdims=True) + RMS_EPS)) * f64(g_norm)
    uv = av_norm * u
    return (mxq(uv, 2, "e4m3") @ unpack4(Wf_words, Wf_scales)) + f64(b_out)


def e4m3fn_bytes(y):
    return np.clip(np.asarray(y, np.float64), -448.0, 448.0).astype(np.float32).astype(ml_dtypes.float8_e4m3fn).view(np.uint8)


def e4m3fn_values(b):
    return np.asarray(b, np.uint8).view(ml_dtypes.float8_e4m3fn).astype(np.float64)


def setup_inputs():
    d = draw0()
    x0 = np.asarray(d['x']).astype(np.float64)
    s = (np.max(np.abs(x0), axis=(0, 1), keepdims=True) / 448.0).astype(np.float32)
    out = {}
    for k, v in d.items():
        if k == 'x':
            out['x_bytes'] = e4m3fn_bytes(x0 / s.astype(np.float64))
            out['x_scale'] = s
        else:
            out[k] = v
    return out


def reference(x_bytes, x_scale, h_attn, Wu_words, Wu_scales, bu, g_norm, Wf_words, Wf_scales, b_out):
    return core(e4m3fn_values(x_bytes) * x_scale.astype(np.float64), h_attn, Wu_words, Wu_scales, bu, g_norm, Wf_words, Wf_scales, b_out)

@@ -1,0 +1,332 @@
+from contextlib import ExitStack
+
+import concourse.mybir as mybir
+from concourse.masks import make_identity
+
+P = 128
+K = 512
+PACK = 4
+GROUP = 512
+TILES = GROUP // P
+EPS = 1.1920928955078125e-07
+TOKENS = 8192
+
+FLOPS = 2 * 2 * TOKENS * K * K
+
+F32 = mybir.dt.float32
+BF16 = mybir.dt.bfloat16
+I32 = mybir.dt.int32
+U32 = mybir.dt.uint32
+U8 = mybir.dt.uint8
+F8 = mybir.dt.float8_e4m3fn
+F8X4 = mybir.dt.float8_e4m3fn_x4
+F4X4 = mybir.dt.float4_e2m1fn_x4
+MULT = mybir.AluOpType.mult
+ADD = mybir.AluOpType.add
+POW = mybir.AluOpType.pow
+ACT = mybir.ActivationFunctionType
+
+
+def tile_hstu_pb_t_w4_kernel(
+    tc, x_bytes, x_scale, h_attn, wu_words, wu_scales, bu, g_norm, wf_words, wf_scales, b_out, out
+):
+    nc = tc.nc
+    groups = TOKENS // GROUP
+
+    x_hbm = x_bytes.flatten_outer_dims().rearrange("(g p j) k -> g p j k", p=P, j=TILES)
+    h_hbm = h_attn.flatten_outer_dims().rearrange("(g p j) k -> g p j k", p=P, j=TILES)
+    o_hbm = out.flatten_outer_dims().rearrange("(g p j) k -> g p j k", p=P, j=TILES)
+
+    with ExitStack() as ctx:
+        const = ctx.enter_context(tc.tile_pool(name="const", bufs=1))
+        raw = ctx.enter_context(tc.tile_pool(name="raw", bufs=6))
+        two = ctx.enter_context(tc.tile_pool(name="two", bufs=2))
+        three = ctx.enter_context(tc.tile_pool(name="three", bufs=3))
+        psum = ctx.enter_context(tc.psum_pool(name="psum", bufs=2))
+
+        ident = const.tile([P, P], F32, name="ident")
+        neg_half = const.tile([P, TILES], F32, name="neg_half")
+        warm = const.tile([P, 1], F32, name="warm")
+        x_scales = const.tile([P, PACK], F32, name="x_scales")
+        bias_raw = const.tile([P, PACK], BF16, name="bias_raw")
+        gain_raw = const.tile([P, PACK], BF16, name="gain_raw")
+        bias_u = const.tile([P, PACK], F32, name="bias_u")
+        gain = const.tile([P, PACK], F32, name="gain")
+        bias_out = const.tile([P, K], BF16, name="bias_out")
+        wu_raw = const.tile([P, 2 * K], U8, name="wu_raw", align_bytes=64)
+        wus_raw = const.tile([P, K], U8, name="wus_raw", align_bytes=64)
+        wu = const.tile([P, 2 * K], U8, name="wu", align_bytes=64)
+        wus = const.tile([P, K], U8, name="wus", align_bytes=64)
+        wf = const.tile([P, 2 * K], U8, name="wf", align_bytes=64)
+        wfs = const.tile([P, K], U8, name="wfs", align_bytes=64)
+
+        st = {}
+
+        def ok(g):
+            return 0 <= g < groups
+
+        def load_x(g):
+            if ok(g):
+                xr = raw.tile([P, TILES * K], U8, name="xr", align_bytes=64)
+                nc.sync.dma_start(out=xr[:], in_=x_hbm[g].rearrange("p j k -> p (j k)"))
+                st["xr", g] = xr
+
+        def load_h(g):
+            if ok(g):
+                h = raw.tile([P, TILES, K], BF16, name="h", align_bytes=64)
+                nc.sync.dma_start(out=h[:], in_=h_hbm[g])
+                st["h", g] = h
+
+        def cast_x(g, half):
+            if ok(g):
+                if half == 0:
+                    xb = three.tile([P, TILES * K], BF16, name="xb", align_bytes=64)
+                    st["xb", g] = xb
+                cols = slice(half * 2 * K, (half + 1) * 2 * K)
+                nc.scalar.copy(out=st["xb", g][:, cols], in_=st["xr", g][:, cols].bitcast(F8))
+
+        def turn_x(g, half):
+            if ok(g):
+                xt = psum.tile([P, 2, 2 * P], F32, name="xt")
+                words = st["xb", g][:].bitcast(F32)
+                for i in range(2):
+                    base = (half * 2 + i) * (K // 2)
+                    for u in range(2):
+                        nc.tensor.transpose(
+                            xt[:, u, i * P : (i + 1) * P], words[:, base + u : base + K // 2 : 2], ident[:]
+                        )
+                st["xt", g, half] = xt
+
+        def scale_x(g, half):
+            if ok(g):
+                if half == 0:
+                    xi = two.tile([P, GROUP * PACK], BF16, name="xi", align_bytes=64)
+                    st["xi", g] = xi
+                cols = slice(half * 1024, (half + 1) * 1024)
+                nc.vector.tensor_tensor(
+                    out=st["xi", g][:, cols].rearrange("p (k u e) -> p k u e", u=2, e=2),
+                    in0=st["xt", g, half][:]
+                    .rearrange("p u k -> p (u k)")
+                    .bitcast(BF16)
+                    .rearrange("p (u k e) -> p k u e", u=2, e=2),
+                    in1=x_scales[:].rearrange("p (o u e) -> p o u e", o=1, u=2).to_broadcast([P, 256, 2, 2]),
+                    op=MULT,
+                )
+
+        def quant_x(g):
+            if ok(g):
+                xc = three.tile([P, GROUP], U32, name="xc", align_bytes=64)
+                xs = three.tile([P, GROUP], U8, name="xs", align_bytes=64)
+                nc.vector.quantize_mx(out=xc[:].bitcast(F8X4), scales=xs[:], in_=st["xi", g][:])
+                st["xc", g], st["xs", g] = xc, xs
+
+        def mm_z(g, t):
+            if ok(g):
+                z = psum.tile([P, GROUP], F32, name="z")
+                nc.tensor.matmul_mx(
+                    out=z[:],
+                    lhsT=wu[:, t * 256 : (t + 1) * 256].bitcast(F4X4),
+                    lhsT_scale=wus[:, t * P : (t + 1) * P],
+                    rhs=st["xc", g][:].bitcast(F8X4),
+                    rhs_scale=st["xs", g][:],
+                    start=True,
+                    stop=True,
+                )
+                st["z", g, t] = z
+
+        def silu(g, t):
+            if ok(g):
+                if t == 0:
+                    ut = three.tile([P, PACK, GROUP], F32, name="ut", align_bytes=64)
+                    st["ut", g] = ut
+                nc.scalar.activation(
+                    out=st["ut", g][:, t, :], in_=st["z", g, t][:], func=ACT.Silu, bias=bias_u[:, t : t + 1]
+                )
+
+        def times_gain(g, t):
+            if ok(g):
+                nc.gpsimd.tensor_scalar(
+                    out=st["ut", g][:, t, :],
+                    in0=st["ut", g][:, t, :],
+                    scalar1=gain[:, t : t + 1],
+                    scalar2=0.0,
+                    op0=MULT,
+                    op1=ADD,
+                )
+
+        def square(g, j):
+            if ok(g):
+                if j == 0:
+                    ssq = three.tile([P, TILES], F32, name="ssq")
+                    st["ssq", g] = ssq
+                junk = two.tile([P, K], BF16, name="junk")
+                nc.scalar.activation(
+                    out=junk[:], in_=st["h", g][:, j, :], func=ACT.Square, accum_out=st["ssq", g][:, j : j + 1]
+                )
+
+        def inv_rms(g):
+            if ok(g):
+                ms = three.tile([P, TILES], F32, name="ms")
+                rstd = three.tile([P, TILES], F32, name="rstd")
+                nc.gpsimd.tensor_scalar(
+                    out=ms[:], in0=st["ssq", g][:], scalar1=1.0 / K, scalar2=EPS, op0=MULT, op1=ADD
+                )
+                nc.gpsimd.tensor_tensor(out=rstd[:], in0=ms[:], in1=neg_half[:], op=POW)
+                st["rstd", g] = rstd
+
+        def norm(g, j):
+            if ok(g):
+                if j == 0:
+                    n = two.tile([P, TILES, PACK, P], F32, name="n", align_bytes=64)
+                    st["n", g] = n
+                nc.gpsimd.tensor_scalar(
+                    out=st["n", g][:, j],
+                    in0=st["h", g][:, j, :].rearrange("p (q t) -> p t q", t=PACK),
+                    scalar1=st["rstd", g][:, j : j + 1],
+                    scalar2=0.0,
+                    op0=MULT,
+                    op1=ADD,
+                )
+
+        def turn_n(g, j):
+            if ok(g):
+                nt = psum.tile([P, PACK, P], F32, name="nt")
+                for t in range(PACK):
+                    nc.tensor.transpose(nt[:, t, :], st["n", g][:, j, t, :], ident[:])
+                st["nt", g, j] = nt
+
+        def gate(g, j):
+            if ok(g):
+                if j == 0:
+                    uv = two.tile([P, GROUP * PACK], BF16, name="uv", align_bytes=64)
+                    st["uv", g] = uv
+                nc.vector.tensor_tensor(
+                    out=st["uv", g][:, j * K : (j + 1) * K].rearrange("p (q t) -> p q t", t=PACK),
+                    in0=st["nt", g, j][:].rearrange("p t q -> p q t"),
+                    in1=st["ut", g][:, :, j * P : (j + 1) * P].rearrange("p t q -> p q t"),
+                    op=MULT,
+                )
+
+        def quant_uv(g):
+            if ok(g):
+                uc = two.tile([P, GROUP], U32, name="uc", align_bytes=64)
+                us = two.tile([P, GROUP], U8, name="us", align_bytes=64)
+                nc.vector.quantize_mx(out=uc[:].bitcast(F8X4), scales=us[:], in_=st["uv", g][:])
+                st["uc", g], st["us", g] = uc, us
+
+        def mm_o(g, j):
+            if ok(g):
+                o = psum.tile([P, K], F32, name="o")
+                cols = slice(j * P, (j + 1) * P)
+                nc.tensor.matmul_mx(
+                    out=o[:],
+                    lhsT=st["uc", g][:, cols].bitcast(F8X4),
+                    lhsT_scale=st["us", g][:, cols],
+                    rhs=wf[:].bitcast(F4X4),
+                    rhs_scale=wfs[:],
+                    start=True,
+                    stop=True,
+                )
+                st["o", g, j] = o
+
+        def add_bias(g, j):
+            if ok(g):
+                if j == 0:
+                    res = three.tile([P, TILES, K], F32, name="res", align_bytes=64)
+                    st["res", g] = res
+                nc.vector.tensor_tensor(out=st["res", g][:, j, :], in0=st["o", g, j][:], in1=bias_out[:], op=ADD)
+
+        def store(g):
+            if ok(g):
+                nc.sync.dma_start(out=o_hbm[g], in_=st["res", g][:])
+
+        with tc.manual_schedule():
+            nc.vector.memset(warm[:], 0.0)
+            nc.scalar.activation(out=warm[:], in_=warm[:], func=ACT.Silu)
+            nc.vector.memset(wus_raw[:].bitcast(I32), 0)
+            nc.vector.memset(wfs[:].bitcast(I32), 0)
+            nc.vector.memset(neg_half[:], -0.5)
+            make_identity(nc, ident[:])
+
+            load_x(0)
+            nc.sync.dma_start(out=x_scales[:], in_=x_scale.rearrange("a b (p t) -> p (a b t)", t=PACK))
+            load_h(0)
+            nc.sync.dma_start(out=wu_raw[:], in_=wu_words[0])
+            for q in range(4):
+                nc.sync.dma_start(
+                    out=wus_raw[32 * q : 32 * q + 4, :].bitcast(I32), in_=wu_scales[0, 4 * q : 4 * q + 4, :].bitcast(I32)
+                )
+            nc.sync.dma_start(out=bias_raw[:], in_=bu.rearrange("(p t) -> p t", t=PACK))
+            nc.sync.dma_start(out=gain_raw[:], in_=g_norm.rearrange("(p t) -> p t", t=PACK))
+            load_x(1)
+            load_h(1)
+            nc.sync.dma_start(out=wf[:], in_=wf_words[0])
+            for q in range(4):
+                nc.sync.dma_start(
+                    out=wfs[32 * q : 32 * q + 4, :].bitcast(I32), in_=wf_scales[0, 4 * q : 4 * q + 4, :].bitcast(I32)
+                )
+            nc.sync.dma_start(out=bias_out[:], in_=b_out.partition_broadcast(P))
+            for g in range(2, 5):
+                load_x(g)
+                load_h(g)
+
+            nc.vector.tensor_copy(
+                out=wu[:].rearrange("p (t m b) -> p t m b", t=PACK, b=2),
+                in_=wu_raw[:].rearrange("p (m t b) -> p t m b", t=PACK, b=2),
+            )
+            nc.vector.tensor_copy(
+                out=wus[:].rearrange("p (t m) -> p t m", t=PACK), in_=wus_raw[:].rearrange("p (m t) -> p t m", t=PACK)
+            )
+            nc.vector.tensor_copy(out=bias_u[:], in_=bias_raw[:])
+            nc.vector.tensor_copy(out=gain[:], in_=gain_raw[:])
+
+            for s in range(-4, groups + 1):
+                if s > -1:
+                    load_x(s + 5)
+                    load_h(s + 5)
+                mm_o(s - 1, 0)
+                mm_o(s - 1, 1)
+                mm_z(s + 1, 0)
+                mm_z(s + 1, 1)
+                silu(s + 1, 0)
+                silu(s + 1, 1)
+                gate(s, 0)
+                scale_x(s + 2, 0)
+                gate(s, 1)
+                norm(s + 1, 0)
+                norm(s + 1, 1)
+                turn_n(s, 2)
+                turn_n(s, 3)
+                times_gain(s + 1, 0)
+                times_gain(s + 1, 1)
+                turn_x(s + 3, 0)
+                add_bias(s - 1, 0)
+                scale_x(s + 2, 1)
+                square(s + 2, 0)
+                square(s + 2, 1)
+                cast_x(s + 4, 0)
+                gate(s, 2)
+                add_bias(s - 1, 1)
+                mm_z(s + 1, 2)
+                mm_z(s + 1, 3)
+                mm_o(s - 1, 2)
+                mm_o(s - 1, 3)
+                silu(s + 1, 2)
+                silu(s + 1, 3)
+                norm(s + 1, 2)
+                norm(s + 1, 3)
+                times_gain(s + 1, 2)
+                times_gain(s + 1, 3)
+                square(s + 2, 2)
+                square(s + 2, 3)
+                cast_x(s + 4, 1)
+                turn_x(s + 3, 1)
+                quant_x(s + 2)
+                turn_n(s + 1, 0)
+                gate(s, 3)
+                turn_n(s + 1, 1)
+                add_bias(s - 1, 2)
+                quant_uv(s)
+                add_bias(s - 1, 3)
+                store(s - 1)
+                inv_rms(s + 2)

@@ -8,6 +8,7 @@ K = 512
 PACK = 4
 GROUP = 512
 TILES = GROUP // P
+RUN = 4
 EPS = 1.1920928955078125e-07
 TOKENS = 8192
 
@@ -62,183 +63,179 @@ def tile_hstu_pb_t_w4_kernel(
 
         st = {}
 
-        def ok(g):
-            return 0 <= g < groups
+        issued = set()
 
-        def load_x(g):
-            if ok(g):
+        def once(step, *which):
+            if 0 <= which[0] < groups and (step, which) not in issued:
+                issued.add((step, which))
+                step(*which)
+
+        def load_x(g, half):
+            if half == 0:
                 xr = raw.tile([P, TILES * K], U8, name="xr", align_bytes=64)
-                nc.sync.dma_start(out=xr[:], in_=x_hbm[g].rearrange("p j k -> p (j k)"))
                 st["xr", g] = xr
+            cols = slice(half * 2 * K, (half + 1) * 2 * K)
+            nc.sync.dma_start(out=st["xr", g][:, cols], in_=x_hbm[g].rearrange("p j k -> p (j k)")[:, cols])
 
         def load_h(g):
-            if ok(g):
-                h = raw.tile([P, TILES, K], BF16, name="h", align_bytes=64)
-                nc.sync.dma_start(out=h[:], in_=h_hbm[g])
-                st["h", g] = h
+            h = raw.tile([P, TILES, K], BF16, name="h", align_bytes=64)
+            nc.sync.dma_start(out=h[:], in_=h_hbm[g])
+            st["h", g] = h
 
         def cast_x(g, half):
-            if ok(g):
-                if half == 0:
-                    xb = three.tile([P, TILES * K], BF16, name="xb", align_bytes=64)
-                    st["xb", g] = xb
-                cols = slice(half * 2 * K, (half + 1) * 2 * K)
-                nc.scalar.copy(out=st["xb", g][:, cols], in_=st["xr", g][:, cols].bitcast(F8))
+            if half == 0:
+                xb = three.tile([P, TILES * K], BF16, name="xb", align_bytes=64)
+                st["xb", g] = xb
+            cols = slice(half * 2 * K, (half + 1) * 2 * K)
+            nc.scalar.copy(out=st["xb", g][:, cols], in_=st["xr", g][:, cols].bitcast(F8))
 
         def turn_x(g, half):
-            if ok(g):
-                xt = psum.tile([P, 2, 2 * P], F32, name="xt")
-                words = st["xb", g][:].bitcast(F32)
-                for i in range(2):
-                    base = (half * 2 + i) * (K // 2)
-                    for u in range(2):
-                        nc.tensor.transpose(
-                            xt[:, u, i * P : (i + 1) * P], words[:, base + u : base + K // 2 : 2], ident[:]
-                        )
-                st["xt", g, half] = xt
+            xt = psum.tile([P, 2, 2 * P], F32, name="xt")
+            words = st["xb", g][:].bitcast(F32)
+            for i in range(2):
+                base = (half * 2 + i) * (K // 2)
+                for u in range(2):
+                    nc.tensor.transpose(
+                        xt[:, u, i * P : (i + 1) * P], words[:, base + u : base + K // 2 : 2], ident[:]
+                    )
+            st["xt", g, half] = xt
 
         def scale_x(g, half):
-            if ok(g):
-                if half == 0:
-                    xi = two.tile([P, GROUP * PACK], BF16, name="xi", align_bytes=64)
-                    st["xi", g] = xi
-                cols = slice(half * 1024, (half + 1) * 1024)
-                nc.vector.tensor_tensor(
-                    out=st["xi", g][:, cols].rearrange("p (k u e) -> p k u e", u=2, e=2),
-                    in0=st["xt", g, half][:]
-                    .rearrange("p u k -> p (u k)")
-                    .bitcast(BF16)
-                    .rearrange("p (u k e) -> p k u e", u=2, e=2),
-                    in1=x_scales[:].rearrange("p (o u e) -> p o u e", o=1, u=2).to_broadcast([P, 256, 2, 2]),
-                    op=MULT,
-                )
+            if half == 0:
+                xi = two.tile([P, GROUP * PACK], BF16, name="xi", align_bytes=64)
+                st["xi", g] = xi
+            cols = slice(half * 1024, (half + 1) * 1024)
+            nc.vector.tensor_tensor(
+                out=st["xi", g][:, cols].rearrange("p (k u e) -> p k u e", u=2, e=2),
+                in0=st["xt", g, half][:]
+                .rearrange("p u k -> p (u k)")
+                .bitcast(BF16)
+                .rearrange("p (u k e) -> p k u e", u=2, e=2),
+                in1=x_scales[:].rearrange("p (o u e) -> p o u e", o=1, u=2).to_broadcast([P, 256, 2, 2]),
+                op=MULT,
+            )
 
         def quant_x(g):
-            if ok(g):
-                xc = three.tile([P, GROUP], U32, name="xc", align_bytes=64)
-                xs = three.tile([P, GROUP], U8, name="xs", align_bytes=64)
-                nc.vector.quantize_mx(out=xc[:].bitcast(F8X4), scales=xs[:], in_=st["xi", g][:])
-                st["xc", g], st["xs", g] = xc, xs
+            xc = three.tile([P, GROUP], U32, name="xc", align_bytes=64)
+            xs = three.tile([P, GROUP], U8, name="xs", align_bytes=64)
+            nc.vector.quantize_mx(out=xc[:].bitcast(F8X4), scales=xs[:], in_=st["xi", g][:])
+            st["xc", g], st["xs", g] = xc, xs
 
         def mm_z(g, t):
-            if ok(g):
-                z = psum.tile([P, GROUP], F32, name="z")
-                nc.tensor.matmul_mx(
-                    out=z[:],
-                    lhsT=wu[:, t * 256 : (t + 1) * 256].bitcast(F4X4),
-                    lhsT_scale=wus[:, t * P : (t + 1) * P],
-                    rhs=st["xc", g][:].bitcast(F8X4),
-                    rhs_scale=st["xs", g][:],
-                    start=True,
-                    stop=True,
-                )
-                st["z", g, t] = z
+            z = psum.tile([P, GROUP], F32, name="z")
+            nc.tensor.matmul_mx(
+                out=z[:],
+                lhsT=wu[:, t * 256 : (t + 1) * 256].bitcast(F4X4),
+                lhsT_scale=wus[:, t * P : (t + 1) * P],
+                rhs=st["xc", g][:].bitcast(F8X4),
+                rhs_scale=st["xs", g][:],
+                start=True,
+                stop=True,
+            )
+            st["z", g, t] = z
 
         def silu(g, t):
-            if ok(g):
-                if t == 0:
-                    ut = three.tile([P, PACK, GROUP], F32, name="ut", align_bytes=64)
-                    st["ut", g] = ut
-                nc.scalar.activation(
-                    out=st["ut", g][:, t, :], in_=st["z", g, t][:], func=ACT.Silu, bias=bias_u[:, t : t + 1]
-                )
+            if t == 0:
+                ut = three.tile([P, PACK, GROUP], F32, name="ut", align_bytes=64)
+                st["ut", g] = ut
+            nc.scalar.activation(
+                out=st["ut", g][:, t, :], in_=st["z", g, t][:], func=ACT.Silu, bias=bias_u[:, t : t + 1]
+            )
 
         def times_gain(g, t):
-            if ok(g):
-                nc.gpsimd.tensor_scalar(
-                    out=st["ut", g][:, t, :],
-                    in0=st["ut", g][:, t, :],
-                    scalar1=gain[:, t : t + 1],
-                    scalar2=0.0,
-                    op0=MULT,
-                    op1=ADD,
-                )
+            engine = nc.vector if g == 0 else nc.gpsimd
+            engine.tensor_scalar(
+                out=st["ut", g][:, t, :],
+                in0=st["ut", g][:, t, :],
+                scalar1=gain[:, t : t + 1],
+                scalar2=0.0,
+                op0=MULT,
+                op1=ADD,
+            )
 
         def square(g, j):
-            if ok(g):
-                if j == 0:
-                    ssq = three.tile([P, TILES], F32, name="ssq")
-                    st["ssq", g] = ssq
-                junk = two.tile([P, K], BF16, name="junk")
-                nc.scalar.activation(
-                    out=junk[:], in_=st["h", g][:, j, :], func=ACT.Square, accum_out=st["ssq", g][:, j : j + 1]
-                )
+            if j == 0:
+                ssq = three.tile([P, TILES], F32, name="ssq")
+                st["ssq", g] = ssq
+            junk = two.tile([P, K], BF16, name="junk")
+            nc.scalar.activation(
+                out=junk[:], in_=st["h", g][:, j, :], func=ACT.Square, accum_out=st["ssq", g][:, j : j + 1]
+            )
 
         def inv_rms(g):
-            if ok(g):
-                ms = three.tile([P, TILES], F32, name="ms")
-                rstd = three.tile([P, TILES], F32, name="rstd")
-                nc.gpsimd.tensor_scalar(
-                    out=ms[:], in0=st["ssq", g][:], scalar1=1.0 / K, scalar2=EPS, op0=MULT, op1=ADD
-                )
-                nc.gpsimd.tensor_tensor(out=rstd[:], in0=ms[:], in1=neg_half[:], op=POW)
-                st["rstd", g] = rstd
+            ms = three.tile([P, TILES], F32, name="ms")
+            rstd = three.tile([P, TILES], F32, name="rstd")
+            nc.gpsimd.tensor_scalar(
+                out=ms[:], in0=st["ssq", g][:], scalar1=1.0 / K, scalar2=EPS, op0=MULT, op1=ADD
+            )
+            nc.gpsimd.tensor_tensor(out=rstd[:], in0=ms[:], in1=neg_half[:], op=POW)
+            st["rstd", g] = rstd
 
         def norm(g, j):
-            if ok(g):
-                if j == 0:
-                    n = two.tile([P, TILES, PACK, P], F32, name="n", align_bytes=64)
-                    st["n", g] = n
-                nc.gpsimd.tensor_scalar(
-                    out=st["n", g][:, j],
-                    in0=st["h", g][:, j, :].rearrange("p (q t) -> p t q", t=PACK),
-                    scalar1=st["rstd", g][:, j : j + 1],
-                    scalar2=0.0,
-                    op0=MULT,
-                    op1=ADD,
-                )
+            if j == 0:
+                n = two.tile([P, TILES, PACK, P], F32, name="n", align_bytes=64)
+                st["n", g] = n
+            engine = nc.vector if g in (0, groups - 1) else nc.gpsimd
+            engine.tensor_scalar(
+                out=st["n", g][:, j],
+                in0=st["h", g][:, j, :].rearrange("p (q t) -> p t q", t=PACK),
+                scalar1=st["rstd", g][:, j : j + 1],
+                scalar2=0.0,
+                op0=MULT,
+                op1=ADD,
+            )
 
         def turn_n(g, j):
-            if ok(g):
-                nt = psum.tile([P, PACK, P], F32, name="nt")
-                for t in range(PACK):
-                    nc.tensor.transpose(nt[:, t, :], st["n", g][:, j, t, :], ident[:])
-                st["nt", g, j] = nt
+            nt = psum.tile([P, PACK, P], F32, name="nt")
+            for t in range(PACK):
+                nc.tensor.transpose(nt[:, t, :], st["n", g][:, j, t, :], ident[:])
+            st["nt", g, j] = nt
 
         def gate(g, j):
-            if ok(g):
-                if j == 0:
-                    uv = two.tile([P, GROUP * PACK], BF16, name="uv", align_bytes=64)
-                    st["uv", g] = uv
-                nc.vector.tensor_tensor(
-                    out=st["uv", g][:, j * K : (j + 1) * K].rearrange("p (q t) -> p q t", t=PACK),
-                    in0=st["nt", g, j][:].rearrange("p t q -> p q t"),
-                    in1=st["ut", g][:, :, j * P : (j + 1) * P].rearrange("p t q -> p q t"),
-                    op=MULT,
-                )
+            if j == 0:
+                uv = two.tile([P, GROUP * PACK], BF16, name="uv", align_bytes=64)
+                st["uv", g] = uv
+            nc.vector.tensor_tensor(
+                out=st["uv", g][:, j * K : (j + 1) * K].rearrange("p (c i t) -> p c t i", i=RUN, t=PACK),
+                in0=st["nt", g, j][:].rearrange("p t (c i) -> p c t i", i=RUN),
+                in1=st["ut", g][:, :, j * P : (j + 1) * P].rearrange("p t (c i) -> p c t i", i=RUN),
+                op=MULT,
+            )
 
-        def quant_uv(g):
-            if ok(g):
+        def quant_uv(g, first, last):
+            if first == 0:
                 uc = two.tile([P, GROUP], U32, name="uc", align_bytes=64)
                 us = two.tile([P, GROUP], U8, name="us", align_bytes=64)
-                nc.vector.quantize_mx(out=uc[:].bitcast(F8X4), scales=us[:], in_=st["uv", g][:])
                 st["uc", g], st["us", g] = uc, us
+            cols = slice(first * P, last * P)
+            nc.vector.quantize_mx(
+                out=st["uc", g][:, cols].bitcast(F8X4),
+                scales=st["us", g][:, cols],
+                in_=st["uv", g][:, first * K : last * K],
+            )
 
         def mm_o(g, j):
-            if ok(g):
-                o = psum.tile([P, K], F32, name="o")
-                cols = slice(j * P, (j + 1) * P)
-                nc.tensor.matmul_mx(
-                    out=o[:],
-                    lhsT=st["uc", g][:, cols].bitcast(F8X4),
-                    lhsT_scale=st["us", g][:, cols],
-                    rhs=wf[:].bitcast(F4X4),
-                    rhs_scale=wfs[:],
-                    start=True,
-                    stop=True,
-                )
-                st["o", g, j] = o
+            o = psum.tile([P, K], F32, name="o")
+            cols = slice(j * P, (j + 1) * P)
+            nc.tensor.matmul_mx(
+                out=o[:],
+                lhsT=st["uc", g][:, cols].bitcast(F8X4),
+                lhsT_scale=st["us", g][:, cols],
+                rhs=wf[:].bitcast(F4X4),
+                rhs_scale=wfs[:],
+                start=True,
+                stop=True,
+            )
+            st["o", g, j] = o
 
         def add_bias(g, j):
-            if ok(g):
-                if j == 0:
-                    res = three.tile([P, TILES, K], F32, name="res", align_bytes=64)
-                    st["res", g] = res
-                nc.vector.tensor_tensor(out=st["res", g][:, j, :], in0=st["o", g, j][:], in1=bias_out[:], op=ADD)
+            if j == 0:
+                res = three.tile([P, TILES, K], F32, name="res", align_bytes=64)
+                st["res", g] = res
+            nc.vector.tensor_tensor(out=st["res", g][:, j, :], in0=st["o", g, j][:], in1=bias_out[:], op=ADD)
 
-        def store(g):
-            if ok(g):
-                nc.sync.dma_start(out=o_hbm[g], in_=st["res", g][:])
+        def store(g, first, last):
+            nc.sync.dma_start(out=o_hbm[g][:, first:last], in_=st["res", g][:, first:last])
 
         with tc.manual_schedule():
             nc.vector.memset(warm[:], 0.0)
@@ -248,18 +245,20 @@ def tile_hstu_pb_t_w4_kernel(
             nc.vector.memset(neg_half[:], -0.5)
             make_identity(nc, ident[:])
 
-            load_x(0)
-            nc.sync.dma_start(out=x_scales[:], in_=x_scale.rearrange("a b (p t) -> p (a b t)", t=PACK))
-            load_h(0)
+            once(load_x, 0, 0)
+            once(load_x, 0, 1)
+            nc.scalar.dma_start(out=x_scales[:], in_=x_scale.rearrange("a b (p t) -> p (a b t)", t=PACK))
+            nc.scalar.dma_start(out=bias_raw[:], in_=bu.rearrange("(p t) -> p t", t=PACK))
+            nc.scalar.dma_start(out=gain_raw[:], in_=g_norm.rearrange("(p t) -> p t", t=PACK))
+            once(load_h, 0)
             nc.sync.dma_start(out=wu_raw[:], in_=wu_words[0])
             for q in range(4):
                 nc.sync.dma_start(
                     out=wus_raw[32 * q : 32 * q + 4, :].bitcast(I32), in_=wu_scales[0, 4 * q : 4 * q + 4, :].bitcast(I32)
                 )
-            nc.sync.dma_start(out=bias_raw[:], in_=bu.rearrange("(p t) -> p t", t=PACK))
-            nc.sync.dma_start(out=gain_raw[:], in_=g_norm.rearrange("(p t) -> p t", t=PACK))
-            load_x(1)
-            load_h(1)
+            once(load_x, 1, 0)
+            once(load_x, 1, 1)
+            once(load_h, 1)
             nc.sync.dma_start(out=wf[:], in_=wf_words[0])
             for q in range(4):
                 nc.sync.dma_start(
@@ -267,9 +266,19 @@ def tile_hstu_pb_t_w4_kernel(
                 )
             nc.sync.dma_start(out=bias_out[:], in_=b_out.partition_broadcast(P))
             for g in range(2, 5):
-                load_x(g)
-                load_h(g)
+                once(load_x, g, 0)
+                once(load_x, g, 1)
+                once(load_h, g)
 
+            once(cast_x, 0, 0)
+            once(turn_x, 0, 0)
+            once(cast_x, 0, 1)
+            once(turn_x, 0, 1)
+            for j in range(TILES):
+                once(square, 0, j)
+            once(scale_x, 0, 0)
+            once(scale_x, 0, 1)
+            once(quant_x, 0)
             nc.vector.tensor_copy(
                 out=wu[:].rearrange("p (t m b) -> p t m b", t=PACK, b=2),
                 in_=wu_raw[:].rearrange("p (m t b) -> p t m b", t=PACK, b=2),
@@ -279,54 +288,103 @@ def tile_hstu_pb_t_w4_kernel(
             )
             nc.vector.tensor_copy(out=bias_u[:], in_=bias_raw[:])
             nc.vector.tensor_copy(out=gain[:], in_=gain_raw[:])
-
-            for s in range(-4, groups + 1):
-                if s > -1:
-                    load_x(s + 5)
-                    load_h(s + 5)
-                mm_o(s - 1, 0)
-                mm_o(s - 1, 1)
-                mm_z(s + 1, 0)
-                mm_z(s + 1, 1)
-                silu(s + 1, 0)
-                silu(s + 1, 1)
-                gate(s, 0)
-                scale_x(s + 2, 0)
-                gate(s, 1)
-                norm(s + 1, 0)
-                norm(s + 1, 1)
-                turn_n(s, 2)
-                turn_n(s, 3)
-                times_gain(s + 1, 0)
-                times_gain(s + 1, 1)
-                turn_x(s + 3, 0)
-                add_bias(s - 1, 0)
-                scale_x(s + 2, 1)
-                square(s + 2, 0)
-                square(s + 2, 1)
-                cast_x(s + 4, 0)
-                gate(s, 2)
-                add_bias(s - 1, 1)
-                mm_z(s + 1, 2)
-                mm_z(s + 1, 3)
-                mm_o(s - 1, 2)
-                mm_o(s - 1, 3)
-                silu(s + 1, 2)
-                silu(s + 1, 3)
-                norm(s + 1, 2)
-                norm(s + 1, 3)
-                times_gain(s + 1, 2)
-                times_gain(s + 1, 3)
-                square(s + 2, 2)
-                square(s + 2, 3)
-                cast_x(s + 4, 1)
-                turn_x(s + 3, 1)
-                quant_x(s + 2)
-                turn_n(s + 1, 0)
-                gate(s, 3)
-                turn_n(s + 1, 1)
-                add_bias(s - 1, 2)
-                quant_uv(s)
-                add_bias(s - 1, 3)
-                store(s - 1)
-                inv_rms(s + 2)
+            once(inv_rms, 0)
+            once(cast_x, 1, 0)
+            once(turn_x, 1, 0)
+            for j in range(TILES):
+                once(norm, 0, j)
+            once(turn_n, 0, 0)
+            once(turn_n, 0, 1)
+            once(scale_x, 1, 0)
+            for t in range(PACK):
+                once(mm_z, 0, t)
+                once(silu, 0, t)
+                once(times_gain, 0, t)
+            once(cast_x, 1, 1)
+            once(turn_x, 1, 1)
+            once(scale_x, 1, 1)
+            once(quant_x, 1)
+            for j in range(TILES):
+                once(square, 1, j)
+            once(inv_rms, 1)
+            once(cast_x, 2, 0)
+            once(cast_x, 2, 1)
+            once(turn_x, 2, 0)
+            once(turn_x, 2, 1)
+            for s in range(groups - 1):
+                once(load_x, s + 5, 0)
+                once(load_x, s + 5, 1)
+                once(load_h, s + 5)
+                once(mm_z, s + 1, 0)
+                once(mm_z, s + 1, 1)
+                once(silu, s + 1, 0)
+                once(silu, s + 1, 1)
+                once(mm_o, s - 1, 0)
+                once(mm_o, s - 1, 1)
+                once(times_gain, s + 1, 0)
+                once(norm, s + 1, 0)
+                once(norm, s + 1, 1)
+                once(times_gain, s + 1, 1)
+                once(gate, s, 0)
+                once(gate, s, 1)
+                once(turn_n, s, 2)
+                once(turn_n, s, 3)
+                once(add_bias, s - 1, 0)
+                once(scale_x, s + 2, 0)
+                once(add_bias, s - 1, 1)
+                once(cast_x, s + 3, 0)
+                once(mm_z, s + 1, 2)
+                once(mm_z, s + 1, 3)
+                once(mm_o, s - 1, 2)
+                once(mm_o, s - 1, 3)
+                once(silu, s + 1, 2)
+                once(cast_x, s + 3, 1)
+                once(silu, s + 1, 3)
+                once(norm, s + 1, 2)
+                once(norm, s + 1, 3)
+                once(times_gain, s + 1, 2)
+                once(times_gain, s + 1, 3)
+                once(gate, s, 2)
+                once(scale_x, s + 2, 1)
+                once(turn_x, s + 3, 0)
+                once(turn_x, s + 3, 1)
+                once(turn_n, s + 1, 0)
+                once(gate, s, 3)
+                once(turn_n, s + 1, 1)
+                once(add_bias, s - 1, 2)
+                once(add_bias, s - 1, 3)
+                once(store, s - 1, 0, TILES)
+                once(quant_x, s + 2)
+                once(quant_uv, s, 0, TILES)
+                for j in range(TILES):
+                    once(square, s + 2, j)
+                once(inv_rms, s + 2)
+            g = groups - 1
+            once(mm_o, g - 1, 0)
+            once(mm_o, g - 1, 1)
+            once(gate, g, 0)
+            once(gate, g, 1)
+            once(turn_n, g, 2)
+            once(turn_n, g, 3)
+            once(add_bias, g - 1, 0)
+            once(quant_uv, g, 0, 2)
+            once(add_bias, g - 1, 1)
+            once(mm_o, g - 1, 2)
+            once(mm_o, g - 1, 3)
+            once(gate, g, 2)
+            once(gate, g, 3)
+            once(add_bias, g - 1, 2)
+            once(mm_o, g, 0)
+            once(quant_uv, g, 2, TILES)
+            once(add_bias, g - 1, 3)
+            once(store, g - 1, 0, TILES)
+            once(mm_o, g, 1)
+            once(add_bias, g, 0)
+            once(mm_o, g, 2)
+            once(add_bias, g, 1)
+            once(store, g, 0, 2)
+            once(mm_o, g, 3)
+            once(add_bias, g, 2)
+            once(store, g, 2, 3)
+            once(add_bias, g, 3)
+            once(store, g, 3, TILES)

@@ -3,14 +3,17 @@ from contextlib import ExitStack
 import concourse.mybir as mybir
 from concourse.masks import make_identity
 
+TOKENS = 8192
 P = 128
 K = 512
 PACK = 4
-GROUP = 512
-TILES = GROUP // P
+TILES = 4
+GROUP = TILES * P
 RUN = 4
 EPS = 1.1920928955078125e-07
-TOKENS = 8192
+LIFTED = (3,)
+DIRECT = 3
+NORM_ON_SCALAR = (1, 2,)
 
 FLOPS = 2 * 2 * TOKENS * K * K
 
@@ -27,22 +30,77 @@ ADD = mybir.AluOpType.add
 POW = mybir.AluOpType.pow
 ACT = mybir.ActivationFunctionType
 
+ORDER = (
+    ("gate", 0, 0),
+    ("silu", 1, 1),
+    ("mm_o", -2, 3),
+    ("add_bias", -2, 2),
+    ("times_gain", 1, 0),
+    ("cast_x", 4, 0),
+    ("turn_n", 0, 2),
+    ("scale_x", 3, 0),
+    ("mm_z", 1, 2),
+    ("square", 2, 3),
+    ("times_gain", 1, 1),
+    ("mm_z", 1, 3),
+    ("mm_o", -1, 0),
+    ("silu", 1, 2),
+    ("gate", 0, 1),
+    ("inv_rms", 2, 0),
+    ("norm", 1, 2),
+    ("gate", 0, 2),
+    ("times_gain", 1, 2),
+    ("turn_n", 1, 3),
+    ("silu", 1, 3),
+    ("add_bias", -2, 3),
+    ("turn_n", 1, 0),
+    ("times_gain", 1, 3),
+    ("lift_n", 1, 3),
+    ("turn_x", 3, 1),
+    ("add_bias", -1, 0),
+    ("norm", 1, 1),
+    ("mm_o", -1, 1),
+    ("norm", 2, 3),
+    ("square", 3, 2),
+    ("turn_x", 4, 0),
+    ("quant_x", 2, 0),
+    ("quant_uv", 0, 0),
+    ("square", 3, 1),
+    ("mm_z", 2, 0),
+    ("scale_x", 3, 1),
+    ("gate", 1, 3),
+    ("cast_x", 4, 1),
+    ("mm_o", -1, 2),
+    ("square", 3, 0),
+    ("mm_z", 2, 1),
+    ("add_bias", -1, 1),
+    ("silu", 2, 0),
+    ("turn_n", 1, 1),
+    ("norm", 2, 0),
+    ("load_x", 6, 0),
+    ("load_x", 6, 1),
+    ("load_h", 6, 0),
+)
+
+WEIGHTS_AFTER = ("scale_x", 3, 1)
+
 
 def tile_hstu_pb_t_w4_kernel(
     tc, x_bytes, x_scale, h_attn, wu_words, wu_scales, bu, g_norm, wf_words, wf_scales, b_out, out
 ):
     nc = tc.nc
     groups = TOKENS // GROUP
+    last = groups - 1
 
-    x_hbm = x_bytes.flatten_outer_dims().rearrange("(g p j) k -> g p j k", p=P, j=TILES)
+    x_hbm = x_bytes.flatten_outer_dims().rearrange("(g p j) k -> g p (j k)", p=P, j=TILES)
     h_hbm = h_attn.flatten_outer_dims().rearrange("(g p j) k -> g p j k", p=P, j=TILES)
     o_hbm = out.flatten_outer_dims().rearrange("(g p j) k -> g p j k", p=P, j=TILES)
 
     with ExitStack() as ctx:
         const = ctx.enter_context(tc.tile_pool(name="const", bufs=1))
-        raw = ctx.enter_context(tc.tile_pool(name="raw", bufs=6))
         two = ctx.enter_context(tc.tile_pool(name="two", bufs=2))
         three = ctx.enter_context(tc.tile_pool(name="three", bufs=3))
+        six = ctx.enter_context(tc.tile_pool(name="six", bufs=7))
         psum = ctx.enter_context(tc.psum_pool(name="psum", bufs=2))
 
         ident = const.tile([P, P], F32, name="ident")
@@ -61,181 +119,217 @@ def tile_hstu_pb_t_w4_kernel(
         wf = const.tile([P, 2 * K], U8, name="wf", align_bytes=64)
         wfs = const.tile([P, K], U8, name="wfs", align_bytes=64)
 
-        st = {}
+        made = {}
 
-        issued = set()
+        def tile_of(name, g, pool, shape, dtype):
+            if (name, g) not in made:
+                made[name, g] = pool.tile(shape, dtype, name=name, align_bytes=64)
+            return made[name, g]
 
-        def once(step, *which):
-            if 0 <= which[0] < groups and (step, which) not in issued:
-                issued.add((step, which))
-                step(*which)
+        def codes_of_x(g):
+            return tile_of("x_codes", g, three, [P, GROUP], U32), tile_of("x_planes", g, three, [P, GROUP], U8)
+
+        def codes_of_uv(g):
+            return tile_of("uv_codes", g, two, [P, GROUP], U32), tile_of("uv_planes", g, two, [P, GROUP], U8)
+
+        def x_raw_of(g):
+            return tile_of("x_raw", g, six, [P, TILES * K], U8)
+
+        def h_of(g):
+            return tile_of("h", g, six, [P, TILES, K], BF16)
+
+        def x_wide_of(g):
+            return tile_of("x_wide", g, three, [P, TILES * K], BF16)
+
+        def x_mixed_of(g):
+            return tile_of("x_mixed", g, two, [P, GROUP * PACK], BF16)
+
+        def u_of(g):
+            return tile_of("u", g, three, [P, PACK, GROUP], F32)
+
+        def n_of(g):
+            return tile_of("n", g, two, [P, TILES, PACK, P], F32)
+
+        def uv_of(g):
+            return tile_of("uv", g, two, [P, GROUP * PACK], BF16)
 
         def load_x(g, half):
-            if half == 0:
-                xr = raw.tile([P, TILES * K], U8, name="xr", align_bytes=64)
-                st["xr", g] = xr
             cols = slice(half * 2 * K, (half + 1) * 2 * K)
-            nc.sync.dma_start(out=st["xr", g][:, cols], in_=x_hbm[g].rearrange("p j k -> p (j k)")[:, cols])
+            nc.sync.dma_start(out=x_raw_of(g)[:, cols], in_=x_hbm[g][:, cols])
 
-        def load_h(g):
-            h = raw.tile([P, TILES, K], BF16, name="h", align_bytes=64)
-            nc.sync.dma_start(out=h[:], in_=h_hbm[g])
-            st["h", g] = h
+        def load_h(g, whole):
+            nc.sync.dma_start(out=h_of(g)[:], in_=h_hbm[g])
 
         def cast_x(g, half):
-            if half == 0:
-                xb = three.tile([P, TILES * K], BF16, name="xb", align_bytes=64)
-                st["xb", g] = xb
             cols = slice(half * 2 * K, (half + 1) * 2 * K)
-            nc.scalar.copy(out=st["xb", g][:, cols], in_=st["xr", g][:, cols].bitcast(F8))
+            nc.scalar.copy(out=x_wide_of(g)[:, cols], in_=x_raw_of(g)[:, cols].bitcast(F8))
 
         def turn_x(g, half):
-            xt = psum.tile([P, 2, 2 * P], F32, name="xt")
-            words = st["xb", g][:].bitcast(F32)
+            bank = psum.tile([P, 2, 2 * P], F32, name="xt")
+            made["xt", g, half] = bank
+            words = x_wide_of(g)[:].bitcast(F32)
             for i in range(2):
-                base = (half * 2 + i) * (K // 2)
+                first = (half * 2 + i) * (K // 2)
                 for u in range(2):
                     nc.tensor.transpose(
-                        xt[:, u, i * P : (i + 1) * P], words[:, base + u : base + K // 2 : 2], ident[:]
+                        bank[:, u, i * P : (i + 1) * P], words[:, first + u : first + K // 2 : 2], ident[:]
                     )
-            st["xt", g, half] = xt
 
         def scale_x(g, half):
-            if half == 0:
-                xi = two.tile([P, GROUP * PACK], BF16, name="xi", align_bytes=64)
-                st["xi", g] = xi
-            cols = slice(half * 1024, (half + 1) * 1024)
+            cols = slice(half * 2 * K, (half + 1) * 2 * K)
             nc.vector.tensor_tensor(
-                out=st["xi", g][:, cols].rearrange("p (k u e) -> p k u e", u=2, e=2),
-                in0=st["xt", g, half][:]
+                out=x_mixed_of(g)[:, cols].rearrange("p (k u e) -> p k u e", u=2, e=2),
+                in0=made["xt", g, half][:]
                 .rearrange("p u k -> p (u k)")
                 .bitcast(BF16)
                 .rearrange("p (u k e) -> p k u e", u=2, e=2),
-                in1=x_scales[:].rearrange("p (o u e) -> p o u e", o=1, u=2).to_broadcast([P, 256, 2, 2]),
+                in1=x_scales[:].rearrange("p (o u e) -> p o u e", o=1, u=2).to_broadcast([P, 2 * P, 2, 2]),
                 op=MULT,
             )
 
-        def quant_x(g):
-            xc = three.tile([P, GROUP], U32, name="xc", align_bytes=64)
-            xs = three.tile([P, GROUP], U8, name="xs", align_bytes=64)
-            nc.vector.quantize_mx(out=xc[:].bitcast(F8X4), scales=xs[:], in_=st["xi", g][:])
-            st["xc", g], st["xs", g] = xc, xs
+        def quant_x(g, whole):
+            codes, planes = codes_of_x(g)
+            nc.vector.quantize_mx(out=codes[:].bitcast(F8X4), scales=planes[:], in_=x_mixed_of(g)[:])
 
         def mm_z(g, t):
-            z = psum.tile([P, GROUP], F32, name="z")
+            codes, planes = codes_of_x(g)
+            bank = psum.tile([P, GROUP], F32, name="z")
+            made["z", g, t] = bank
             nc.tensor.matmul_mx(
-                out=z[:],
-                lhsT=wu[:, t * 256 : (t + 1) * 256].bitcast(F4X4),
+                out=bank[:],
+                lhsT=wu[:, t * 2 * P : (t + 1) * 2 * P].bitcast(F4X4),
                 lhsT_scale=wus[:, t * P : (t + 1) * P],
-                rhs=st["xc", g][:].bitcast(F8X4),
-                rhs_scale=st["xs", g][:],
+                rhs=codes[:].bitcast(F8X4),
+                rhs_scale=planes[:],
                 start=True,
                 stop=True,
             )
-            st["z", g, t] = z
 
         def silu(g, t):
-            if t == 0:
-                ut = three.tile([P, PACK, GROUP], F32, name="ut", align_bytes=64)
-                st["ut", g] = ut
             nc.scalar.activation(
-                out=st["ut", g][:, t, :], in_=st["z", g, t][:], func=ACT.Silu, bias=bias_u[:, t : t + 1]
+                out=u_of(g)[:, t, :], in_=made["z", g, t][:], func=ACT.Silu, bias=bias_u[:, t : t + 1]
             )
 
         def times_gain(g, t):
+            cols = u_of(g)[:, t, : DIRECT * P]
             engine = nc.vector if g == 0 else nc.gpsimd
             engine.tensor_scalar(
-                out=st["ut", g][:, t, :],
-                in0=st["ut", g][:, t, :],
-                scalar1=gain[:, t : t + 1],
-                scalar2=0.0,
-                op0=MULT,
-                op1=ADD,
+                out=cols, in0=cols, scalar1=gain[:, t : t + 1], scalar2=0.0, op0=MULT, op1=ADD
             )
 
         def square(g, j):
-            if j == 0:
-                ssq = three.tile([P, TILES], F32, name="ssq")
-                st["ssq", g] = ssq
             junk = two.tile([P, K], BF16, name="junk")
             nc.scalar.activation(
-                out=junk[:], in_=st["h", g][:, j, :], func=ACT.Square, accum_out=st["ssq", g][:, j : j + 1]
+                out=junk[:],
+                in_=h_of(g)[:, j, :],
+                func=ACT.Square,
+                accum_out=tile_of("ssq", g, three, [P, TILES], F32)[:, j : j + 1],
             )
 
-        def inv_rms(g):
+        def inv_rms(g, whole):
             ms = three.tile([P, TILES], F32, name="ms")
-            rstd = three.tile([P, TILES], F32, name="rstd")
             nc.gpsimd.tensor_scalar(
-                out=ms[:], in0=st["ssq", g][:], scalar1=1.0 / K, scalar2=EPS, op0=MULT, op1=ADD
+                out=ms[:], in0=made["ssq", g][:], scalar1=1.0 / K, scalar2=EPS, op0=MULT, op1=ADD
             )
+            rstd = tile_of("rstd", g, three, [P, TILES], F32)
             nc.gpsimd.tensor_tensor(out=rstd[:], in0=ms[:], in1=neg_half[:], op=POW)
-            st["rstd", g] = rstd
 
         def norm(g, j):
-            if j == 0:
-                n = two.tile([P, TILES, PACK, P], F32, name="n", align_bytes=64)
-                st["n", g] = n
-            engine = nc.vector if g in (0, groups - 1) else nc.gpsimd
-            engine.tensor_scalar(
-                out=st["n", g][:, j],
-                in0=st["h", g][:, j, :].rearrange("p (q t) -> p t q", t=PACK),
-                scalar1=st["rstd", g][:, j : j + 1],
-                scalar2=0.0,
-                op0=MULT,
-                op1=ADD,
-            )
+            dst = n_of(g)[:, j]
+            src = h_of(g)[:, j, :].rearrange("p (q t) -> p t q", t=PACK)
+            factor = made["rstd", g][:, j : j + 1]
+            if g in (0, last):
+                nc.vector.tensor_scalar(out=dst, in0=src, scalar1=factor, scalar2=None, op0=MULT)
+            elif j in NORM_ON_SCALAR:
+                nc.scalar.activation(out=dst, in_=src, func=ACT.Copy, scale=factor)
+            else:
+                nc.gpsimd.tensor_scalar(out=dst, in0=src, scalar1=factor, scalar2=0.0, op0=MULT, op1=ADD)
 
         def turn_n(g, j):
-            nt = psum.tile([P, PACK, P], F32, name="nt")
+            bank = psum.tile([P, PACK, P], F32, name="nt")
+            made["nt", g, j] = bank
             for t in range(PACK):
-                nc.tensor.transpose(nt[:, t, :], st["n", g][:, j, t, :], ident[:])
-            st["nt", g, j] = nt
+                nc.tensor.transpose(bank[:, t, :], n_of(g)[:, j, t, :], ident[:])
+
+        def lift_n(g, j):
+            lifted = two.tile([P, PACK, P], F32, name="lifted", align_bytes=64)
+            made["lifted", g, j] = lifted
+            for t in range(PACK):
+                nc.scalar.activation(
+                    out=lifted[:, t, :], in_=made["nt", g, j][:, t, :], func=ACT.Copy, scale=gain[:, t : t + 1]
+                )
 
         def gate(g, j):
-            if j == 0:
-                uv = two.tile([P, GROUP * PACK], BF16, name="uv", align_bytes=64)
-                st["uv", g] = uv
-            nc.vector.tensor_tensor(
-                out=st["uv", g][:, j * K : (j + 1) * K].rearrange("p (c i t) -> p c t i", i=RUN, t=PACK),
-                in0=st["nt", g, j][:].rearrange("p t (c i) -> p c t i", i=RUN),
-                in1=st["ut", g][:, :, j * P : (j + 1) * P].rearrange("p t (c i) -> p c t i", i=RUN),
-                op=MULT,
-            )
+            dst = uv_of(g)[:, j * K : (j + 1) * K]
+            u = u_of(g)[:, :, j * P : (j + 1) * P]
+            if j in LIFTED:
+                nc.gpsimd.tensor_tensor(
+                    out=dst.rearrange("p (q t) -> p q t", t=PACK),
+                    in0=made["lifted", g, j][:].rearrange("p t q -> p q t"),
+                    in1=u.rearrange("p t q -> p q t"),
+                    op=MULT,
+                )
+            else:
+                nc.vector.tensor_tensor(
+                    out=dst.rearrange("p (c i t) -> p c t i", i=RUN, t=PACK),
+                    in0=made["nt", g, j][:].rearrange("p t (c i) -> p c t i", i=RUN),
+                    in1=u.rearrange("p t (c i) -> p c t i", i=RUN),
+                    op=MULT,
+                )
 
-        def quant_uv(g, first, last):
-            if first == 0:
-                uc = two.tile([P, GROUP], U32, name="uc", align_bytes=64)
-                us = two.tile([P, GROUP], U8, name="us", align_bytes=64)
-                st["uc", g], st["us", g] = uc, us
-            cols = slice(first * P, last * P)
-            nc.vector.quantize_mx(
-                out=st["uc", g][:, cols].bitcast(F8X4),
-                scales=st["us", g][:, cols],
-                in_=st["uv", g][:, first * K : last * K],
-            )
+        def quant_uv(g, whole):
+            codes, planes = codes_of_uv(g)
+            nc.vector.quantize_mx(out=codes[:].bitcast(F8X4), scales=planes[:], in_=uv_of(g)[:])
 
         def mm_o(g, j):
-            o = psum.tile([P, K], F32, name="o")
+            codes, planes = codes_of_uv(g)
+            bank = psum.tile([P, K], F32, name="o")
+            made["o", g, j] = bank
             cols = slice(j * P, (j + 1) * P)
             nc.tensor.matmul_mx(
-                out=o[:],
-                lhsT=st["uc", g][:, cols].bitcast(F8X4),
-                lhsT_scale=st["us", g][:, cols],
+                out=bank[:],
+                lhsT=codes[:, cols].bitcast(F8X4),
+                lhsT_scale=planes[:, cols],
                 rhs=wf[:].bitcast(F4X4),
                 rhs_scale=wfs[:],
                 start=True,
                 stop=True,
             )
-            st["o", g, j] = o
 
         def add_bias(g, j):
-            if j == 0:
-                res = three.tile([P, TILES, K], F32, name="res", align_bytes=64)
-                st["res", g] = res
-            nc.vector.tensor_tensor(out=st["res", g][:, j, :], in0=st["o", g, j][:], in1=bias_out[:], op=ADD)
+            res = tile_of("res", g, three, [P, TILES, K], F32)
+            nc.vector.tensor_tensor(out=res[:, j, :], in0=made["o", g, j][:], in1=bias_out[:], op=ADD)
+            if g == last and j % 2 == 1:
+                nc.sync.dma_start(out=o_hbm[g][:, j - 1 : j + 1], in_=res[:, j - 1 : j + 1])
+            elif j == TILES - 1:
+                nc.sync.dma_start(out=o_hbm[g], in_=res[:])
 
-        def store(g, first, last):
-            nc.sync.dma_start(out=o_hbm[g][:, first:last], in_=st["res", g][:, first:last])
+        steps = {
+            "load_x": load_x,
+            "load_h": load_h,
+            "cast_x": cast_x,
+            "turn_x": turn_x,
+            "scale_x": scale_x,
+            "quant_x": quant_x,
+            "mm_z": mm_z,
+            "silu": silu,
+            "times_gain": times_gain,
+            "square": square,
+            "inv_rms": inv_rms,
+            "norm": norm,
+            "turn_n": turn_n,
+            "lift_n": lift_n,
+            "gate": gate,
+            "quant_uv": quant_uv,
+            "mm_o": mm_o,
+            "add_bias": add_bias,
+        }
+        issued = set()
+
+        def issue(step, g, part):
+            if 0 <= g < groups and (step, g, part) not in issued:
+                issued.add((step, g, part))
+                steps[step](g, part)
 
         with tc.manual_schedule():
             nc.vector.memset(warm[:], 0.0)
@@ -245,146 +339,45 @@ def tile_hstu_pb_t_w4_kernel(
             nc.vector.memset(neg_half[:], -0.5)
             make_identity(nc, ident[:])
 
-            once(load_x, 0, 0)
-            once(load_x, 0, 1)
+            issue("load_x", 0, 0)
+            issue("load_x", 0, 1)
             nc.scalar.dma_start(out=x_scales[:], in_=x_scale.rearrange("a b (p t) -> p (a b t)", t=PACK))
             nc.scalar.dma_start(out=bias_raw[:], in_=bu.rearrange("(p t) -> p t", t=PACK))
             nc.scalar.dma_start(out=gain_raw[:], in_=g_norm.rearrange("(p t) -> p t", t=PACK))
-            once(load_h, 0)
+            issue("load_h", 0, 0)
             nc.sync.dma_start(out=wu_raw[:], in_=wu_words[0])
             for q in range(4):
                 nc.sync.dma_start(
-                    out=wus_raw[32 * q : 32 * q + 4, :].bitcast(I32), in_=wu_scales[0, 4 * q : 4 * q + 4, :].bitcast(I32)
+                    out=wus_raw[32 * q : 32 * q + 4, :].bitcast(I32),
+                    in_=wu_scales[0, 4 * q : 4 * q + 4, :].bitcast(I32),
                 )
-            once(load_x, 1, 0)
-            once(load_x, 1, 1)
-            once(load_h, 1)
+            issue("load_x", 1, 0)
+            issue("load_x", 1, 1)
+            issue("load_h", 1, 0)
             nc.sync.dma_start(out=wf[:], in_=wf_words[0])
             for q in range(4):
                 nc.sync.dma_start(
-                    out=wfs[32 * q : 32 * q + 4, :].bitcast(I32), in_=wf_scales[0, 4 * q : 4 * q + 4, :].bitcast(I32)
+                    out=wfs[32 * q : 32 * q + 4, :].bitcast(I32),
+                    in_=wf_scales[0, 4 * q : 4 * q + 4, :].bitcast(I32),
                 )
             nc.sync.dma_start(out=bias_out[:], in_=b_out.partition_broadcast(P))
-            for g in range(2, 5):
-                once(load_x, g, 0)
-                once(load_x, g, 1)
-                once(load_h, g)
+            for g in range(2, 7):
+                issue("load_x", g, 0)
+                issue("load_x", g, 1)
+                issue("load_h", g, 0)
 
-            once(cast_x, 0, 0)
-            once(turn_x, 0, 0)
-            once(cast_x, 0, 1)
-            once(turn_x, 0, 1)
-            for j in range(TILES):
-                once(square, 0, j)
-            once(scale_x, 0, 0)
-            once(scale_x, 0, 1)
-            once(quant_x, 0)
-            nc.vector.tensor_copy(
-                out=wu[:].rearrange("p (t m b) -> p t m b", t=PACK, b=2),
-                in_=wu_raw[:].rearrange("p (m t b) -> p t m b", t=PACK, b=2),
-            )
-            nc.vector.tensor_copy(
-                out=wus[:].rearrange("p (t m) -> p t m", t=PACK), in_=wus_raw[:].rearrange("p (m t) -> p t m", t=PACK)
-            )
-            nc.vector.tensor_copy(out=bias_u[:], in_=bias_raw[:])
-            nc.vector.tensor_copy(out=gain[:], in_=gain_raw[:])
-            once(inv_rms, 0)
-            once(cast_x, 1, 0)
-            once(turn_x, 1, 0)
-            for j in range(TILES):
-                once(norm, 0, j)
-            once(turn_n, 0, 0)
-            once(turn_n, 0, 1)
-            once(scale_x, 1, 0)
-            for t in range(PACK):
-                once(mm_z, 0, t)
-                once(silu, 0, t)
-                once(times_gain, 0, t)
-            once(cast_x, 1, 1)
-            once(turn_x, 1, 1)
-            once(scale_x, 1, 1)
-            once(quant_x, 1)
-            for j in range(TILES):
-                once(square, 1, j)
-            once(inv_rms, 1)
-            once(cast_x, 2, 0)
-            once(cast_x, 2, 1)
-            once(turn_x, 2, 0)
-            once(turn_x, 2, 1)
-            for s in range(groups - 1):
-                once(load_x, s + 5, 0)
-                once(load_x, s + 5, 1)
-                once(load_h, s + 5)
-                once(mm_z, s + 1, 0)
-                once(mm_z, s + 1, 1)
-                once(silu, s + 1, 0)
-                once(silu, s + 1, 1)
-                once(mm_o, s - 1, 0)
-                once(mm_o, s - 1, 1)
-                once(times_gain, s + 1, 0)
-                once(norm, s + 1, 0)
-                once(norm, s + 1, 1)
-                once(times_gain, s + 1, 1)
-                once(gate, s, 0)
-                once(gate, s, 1)
-                once(turn_n, s, 2)
-                once(turn_n, s, 3)
-                once(add_bias, s - 1, 0)
-                once(scale_x, s + 2, 0)
-                once(add_bias, s - 1, 1)
-                once(cast_x, s + 3, 0)
-                once(mm_z, s + 1, 2)
-                once(mm_z, s + 1, 3)
-                once(mm_o, s - 1, 2)
-                once(mm_o, s - 1, 3)
-                once(silu, s + 1, 2)
-                once(cast_x, s + 3, 1)
-                once(silu, s + 1, 3)
-                once(norm, s + 1, 2)
-                once(norm, s + 1, 3)
-                once(times_gain, s + 1, 2)
-                once(times_gain, s + 1, 3)
-                once(gate, s, 2)
-                once(scale_x, s + 2, 1)
-                once(turn_x, s + 3, 0)
-                once(turn_x, s + 3, 1)
-                once(turn_n, s + 1, 0)
-                once(gate, s, 3)
-                once(turn_n, s + 1, 1)
-                once(add_bias, s - 1, 2)
-                once(add_bias, s - 1, 3)
-                once(store, s - 1, 0, TILES)
-                once(quant_x, s + 2)
-                once(quant_uv, s, 0, TILES)
-                for j in range(TILES):
-                    once(square, s + 2, j)
-                once(inv_rms, s + 2)
-            g = groups - 1
-            once(mm_o, g - 1, 0)
-            once(mm_o, g - 1, 1)
-            once(gate, g, 0)
-            once(gate, g, 1)
-            once(turn_n, g, 2)
-            once(turn_n, g, 3)
-            once(add_bias, g - 1, 0)
-            once(quant_uv, g, 0, 2)
-            once(add_bias, g - 1, 1)
-            once(mm_o, g - 1, 2)
-            once(mm_o, g - 1, 3)
-            once(gate, g, 2)
-            once(gate, g, 3)
-            once(add_bias, g - 1, 2)
-            once(mm_o, g, 0)
-            once(quant_uv, g, 2, TILES)
-            once(add_bias, g - 1, 3)
-            once(store, g - 1, 0, TILES)
-            once(mm_o, g, 1)
-            once(add_bias, g, 0)
-            once(mm_o, g, 2)
-            once(add_bias, g, 1)
-            once(store, g, 0, 2)
-            once(mm_o, g, 3)
-            once(add_bias, g, 2)
-            once(store, g, 2, 3)
-            once(add_bias, g, 3)
-            once(store, g, 3, TILES)
+
+            for s in range(-6, groups + 4):
+                for step, ahead, part in ORDER:
+                    issue(step, s + ahead, part)
+                    if (step, ahead, part) == WEIGHTS_AFTER and s + ahead == 0:
+                        nc.vector.tensor_copy(
+                            out=wu[:].rearrange("p (t m b) -> p t m b", t=PACK, b=2),
+                            in_=wu_raw[:].rearrange("p (m t b) -> p t m b", t=PACK, b=2),
+                        )
+                        nc.vector.tensor_copy(
+                            out=wus[:].rearrange("p (t m) -> p t m", t=PACK),
+                            in_=wus_raw[:].rearrange("p (m t) -> p t m", t=PACK),
+                        )
+                        nc.vector.tensor_copy(out=bias_u[:], in_=bias_raw[:])
+                        nc.vector.tensor_copy(out=gain[:], in_=gain_raw[:])

@@ -9,11 +9,8 @@ K = 512
 PACK = 4
 TILES = 4
 GROUP = TILES * P
-RUN = 4
 EPS = 1.1920928955078125e-07
-LIFTED = (3,)
-DIRECT = 3
-NORM_ON_SCALAR = (1, 2,)
+MIXES = 2
 
 FLOPS = 2 * 2 * TOKENS * K * K
 
@@ -31,58 +28,55 @@ POW = mybir.AluOpType.pow
 ACT = mybir.ActivationFunctionType
 
 ORDER = (
-    ("gate", 0, 0),
-    ("silu", 1, 1),
-    ("mm_o", -2, 3),
-    ("add_bias", -2, 2),
-    ("times_gain", 1, 0),
-    ("cast_x", 4, 0),
-    ("turn_n", 0, 2),
-    ("scale_x", 3, 0),
-    ("mm_z", 1, 2),
-    ("square", 2, 3),
-    ("times_gain", 1, 1),
-    ("mm_z", 1, 3),
-    ("mm_o", -1, 0),
-    ("silu", 1, 2),
-    ("gate", 0, 1),
-    ("inv_rms", 2, 0),
-    ("norm", 1, 2),
-    ("gate", 0, 2),
-    ("times_gain", 1, 2),
-    ("turn_n", 1, 3),
-    ("silu", 1, 3),
-    ("add_bias", -2, 3),
-    ("turn_n", 1, 0),
-    ("times_gain", 1, 3),
-    ("lift_n", 1, 3),
-    ("turn_x", 3, 1),
-    ("add_bias", -1, 0),
+    ("quant_x", 0, 0),
+    ("cast_x", 2, 0),
+    ("turn_x", 1, 0),
+    ("quant_uv", -2, 0),
+    ("square", 2, 0),
+    ("turn_x", 1, 1),
+    ("add_bias", -3, 3),
+    ("norm", 1, 0),
+    ("square", 2, 1),
+    ("gate", -1, 2),
     ("norm", 1, 1),
-    ("mm_o", -1, 1),
-    ("norm", 2, 3),
-    ("square", 3, 2),
-    ("turn_x", 4, 0),
-    ("quant_x", 2, 0),
-    ("quant_uv", 0, 0),
-    ("square", 3, 1),
-    ("mm_z", 2, 0),
-    ("scale_x", 3, 1),
-    ("gate", 1, 3),
-    ("cast_x", 4, 1),
-    ("mm_o", -1, 2),
-    ("square", 3, 0),
-    ("mm_z", 2, 1),
-    ("add_bias", -1, 1),
-    ("silu", 2, 0),
-    ("turn_n", 1, 1),
-    ("norm", 2, 0),
-    ("load_x", 6, 0),
-    ("load_x", 6, 1),
-    ("load_h", 6, 0),
+    ("mm_z", 0, 0),
+    ("scale_x", 1, 0),
+    ("mm_z", 0, 1),
+    ("norm", 1, 2),
+    ("mm_o", -2, 0),
+    ("silu", 0, 0),
+    ("mm_o", -2, 1),
+    ("gate", -1, 3),
+    ("silu", 0, 1),
+    ("turn_n", 0, 0),
+    ("square", 2, 2),
+    ("scale_x", 1, 1),
+    ("mix", -1, 0),
+    ("turn_n", 0, 1),
+    ("cast_x", 2, 1),
+    ("add_bias", -2, 0),
+    ("mm_z", 0, 2),
+    ("square", 2, 3),
+    ("mix", -1, 1),
+    ("add_bias", -2, 1),
+    ("mm_o", -2, 2),
+    ("silu", 0, 2),
+    ("gate", 0, 0),
+    ("mm_o", -2, 3),
+    ("norm", 1, 3),
+    ("gate", 0, 1),
+    ("mm_z", 0, 3),
+    ("turn_n", 0, 2),
+    ("add_bias", -2, 2),
+    ("inv_rms", 2, 0),
+    ("silu", 0, 3),
+    ("turn_n", 0, 3),
+    ("load_x", 5, 0),
+    ("load_x", 5, 1),
+    ("load_h", 5, 0),
 )
 
-WEIGHTS_AFTER = ("scale_x", 3, 1)
+WEIGHTS_AFTER = ("scale_x", 1, 1)
 
 
 def tile_hstu_pb_t_w4_kernel(
@@ -100,7 +94,7 @@ def tile_hstu_pb_t_w4_kernel(
         const = ctx.enter_context(tc.tile_pool(name="const", bufs=1))
         two = ctx.enter_context(tc.tile_pool(name="two", bufs=2))
         three = ctx.enter_context(tc.tile_pool(name="three", bufs=3))
-        six = ctx.enter_context(tc.tile_pool(name="six", bufs=7))
+        six = ctx.enter_context(tc.tile_pool(name="six", bufs=6))
         psum = ctx.enter_context(tc.psum_pool(name="psum", bufs=2))
 
         ident = const.tile([P, P], F32, name="ident")
@@ -152,6 +146,9 @@ def tile_hstu_pb_t_w4_kernel(
 
         def uv_of(g):
             return tile_of("uv", g, two, [P, GROUP * PACK], BF16)
+
+        def flat_of(g):
+            return tile_of("uv_flat", g, two, [P, PACK, GROUP], BF16)
 
         def load_x(g, half):
             cols = slice(half * 2 * K, (half + 1) * 2 * K)
@@ -210,13 +207,6 @@ def tile_hstu_pb_t_w4_kernel(
                 out=u_of(g)[:, t, :], in_=made["z", g, t][:], func=ACT.Silu, bias=bias_u[:, t : t + 1]
             )
 
-        def times_gain(g, t):
-            cols = u_of(g)[:, t, : DIRECT * P]
-            engine = nc.vector if g == 0 else nc.gpsimd
-            engine.tensor_scalar(
-                out=cols, in0=cols, scalar1=gain[:, t : t + 1], scalar2=0.0, op0=MULT, op1=ADD
-            )
-
         def square(g, j):
             junk = two.tile([P, K], BF16, name="junk")
             nc.scalar.activation(
@@ -235,47 +225,40 @@ def tile_hstu_pb_t_w4_kernel(
             nc.gpsimd.tensor_tensor(out=rstd[:], in0=ms[:], in1=neg_half[:], op=POW)
 
         def norm(g, j):
-            dst = n_of(g)[:, j]
-            src = h_of(g)[:, j, :].rearrange("p (q t) -> p t q", t=PACK)
-            factor = made["rstd", g][:, j : j + 1]
-            if g in (0, last):
-                nc.vector.tensor_scalar(out=dst, in0=src, scalar1=factor, scalar2=None, op0=MULT)
-            elif j in NORM_ON_SCALAR:
-                nc.scalar.activation(out=dst, in_=src, func=ACT.Copy, scale=factor)
+            nc.gpsimd.tensor_scalar(
+                out=n_of(g)[:, j],
+                in0=h_of(g)[:, j, :].rearrange("p (q t) -> p t q", t=PACK),
+                scalar1=made["rstd", g][:, j : j + 1],
+                scalar2=0.0,
+                op0=MULT,
+                op1=ADD,
+            )
+
+        def turn_n(g, t):
+            bank = psum.tile([P, TILES, P], F32, name="nt")
+            made["nt", g, t] = bank
+            for j in range(TILES):
+                nc.tensor.transpose(bank[:, j, :], n_of(g)[:, j, t, :], ident[:])
+
+        def gate(g, t):
+            nc.vector.scalar_tensor_tensor(
+                out=flat_of(g)[:, t, :],
+                in0=made["nt", g, t][:].rearrange("p j q -> p (j q)"),
+                scalar=gain[:, t : t + 1],
+                in1=u_of(g)[:, t, :],
+                op0=MULT,
+                op1=MULT,
+            )
+
+        def mix(g, part):
+            width = GROUP // MIXES
+            cols = slice(part * width, (part + 1) * width)
+            dst = uv_of(g)[:].rearrange("p (k t) -> p k t", t=PACK)[:, cols]
+            src = flat_of(g)[:, :, cols].rearrange("p t k -> p k t")
+            if g == last:
+                nc.vector.tensor_copy(out=dst, in_=src)
             else:
-                nc.gpsimd.tensor_scalar(out=dst, in0=src, scalar1=factor, scalar2=0.0, op0=MULT, op1=ADD)
-
-        def turn_n(g, j):
-            bank = psum.tile([P, PACK, P], F32, name="nt")
-            made["nt", g, j] = bank
-            for t in range(PACK):
-                nc.tensor.transpose(bank[:, t, :], n_of(g)[:, j, t, :], ident[:])
-
-        def lift_n(g, j):
-            lifted = two.tile([P, PACK, P], F32, name="lifted", align_bytes=64)
-            made["lifted", g, j] = lifted
-            for t in range(PACK):
-                nc.scalar.activation(
-                    out=lifted[:, t, :], in_=made["nt", g, j][:, t, :], func=ACT.Copy, scale=gain[:, t : t + 1]
-                )
-
-        def gate(g, j):
-            dst = uv_of(g)[:, j * K : (j + 1) * K]
-            u = u_of(g)[:, :, j * P : (j + 1) * P]
-            if j in LIFTED:
-                nc.gpsimd.tensor_tensor(
-                    out=dst.rearrange("p (q t) -> p q t", t=PACK),
-                    in0=made["lifted", g, j][:].rearrange("p t q -> p q t"),
-                    in1=u.rearrange("p t q -> p q t"),
-                    op=MULT,
-                )
-            else:
-                nc.vector.tensor_tensor(
-                    out=dst.rearrange("p (c i t) -> p c t i", i=RUN, t=PACK),
-                    in0=made["nt", g, j][:].rearrange("p t (c i) -> p c t i", i=RUN),
-                    in1=u.rearrange("p t (c i) -> p c t i", i=RUN),
-                    op=MULT,
-                )
+                nc.gpsimd.tensor_scalar(out=dst, in0=src, scalar1=1.0, scalar2=0.0, op0=MULT, op1=ADD)
 
         def quant_uv(g, whole):
             codes, planes = codes_of_uv(g)
@@ -299,8 +282,8 @@ def tile_hstu_pb_t_w4_kernel(
         def add_bias(g, j):
             res = tile_of("res", g, three, [P, TILES, K], F32)
             nc.vector.tensor_tensor(out=res[:, j, :], in0=made["o", g, j][:], in1=bias_out[:], op=ADD)
-            if g == last and j % 2 == 1:
-                nc.sync.dma_start(out=o_hbm[g][:, j - 1 : j + 1], in_=res[:, j - 1 : j + 1])
+            if g == last:
+                nc.sync.dma_start(out=o_hbm[g][:, j], in_=res[:, j])
             elif j == TILES - 1:
                 nc.sync.dma_start(out=o_hbm[g], in_=res[:])
 
@@ -313,13 +296,12 @@ def tile_hstu_pb_t_w4_kernel(
             "quant_x": quant_x,
             "mm_z": mm_z,
             "silu": silu,
-            "times_gain": times_gain,
             "square": square,
             "inv_rms": inv_rms,
             "norm": norm,
             "turn_n": turn_n,
-            "lift_n": lift_n,
             "gate": gate,
+            "mix": mix,
             "quant_uv": quant_uv,
             "mm_o": mm_o,
             "add_bias": add_bias,
@@ -361,12 +343,16 @@ def tile_hstu_pb_t_w4_kernel(
                     in_=wf_scales[0, 4 * q : 4 * q + 4, :].bitcast(I32),
                 )
             nc.sync.dma_start(out=bias_out[:], in_=b_out.partition_broadcast(P))
-            for g in range(2, 7):
+            for g in range(2, 6):
                 issue("load_x", g, 0)
                 issue("load_x", g, 1)
                 issue("load_h", g, 0)
 
 
+            issue("cast_x", 0, 0)
+            issue("cast_x", 0, 1)
+            issue("turn_x", 0, 0)
+            issue("turn_x", 0, 1)
             for s in range(-6, groups + 4):
                 for step, ahead, part in ORDER:
                     issue(step, s + ahead, part)

@@ -11,6 +11,7 @@ TILES = 4
 GROUP = TILES * P
 EPS = 1.1920928955078125e-07
 MIXES = 2
+NORM_ON_SCALAR = (3,)
 
 FLOPS = 2 * 2 * TOKENS * K * K
 
@@ -29,48 +30,48 @@ ACT = mybir.ActivationFunctionType
 
 ORDER = (
     ("quant_x", 0, 0),
-    ("cast_x", 2, 0),
-    ("turn_x", 1, 0),
+    ("norm", 0, 3),
+    ("turn_n", -1, 3),
     ("quant_uv", -2, 0),
-    ("square", 2, 0),
-    ("turn_x", 1, 1),
-    ("add_bias", -3, 3),
-    ("norm", 1, 0),
-    ("square", 2, 1),
+    ("cast_x", 2, 0),
     ("gate", -1, 2),
-    ("norm", 1, 1),
-    ("mm_z", 0, 0),
-    ("scale_x", 1, 0),
-    ("mm_z", 0, 1),
-    ("norm", 1, 2),
-    ("mm_o", -2, 0),
-    ("silu", 0, 0),
-    ("mm_o", -2, 1),
+    ("inv_rms", 1, 0),
+    ("mm_o", -3, 2),
+    ("norm", 1, 0),
+    ("mm_o", -3, 3),
     ("gate", -1, 3),
-    ("silu", 0, 1),
-    ("turn_n", 0, 0),
-    ("square", 2, 2),
-    ("scale_x", 1, 1),
+    ("mm_z", 0, 0),
+    ("add_bias", -3, 2),
     ("mix", -1, 0),
-    ("turn_n", 0, 1),
-    ("cast_x", 2, 1),
-    ("add_bias", -2, 0),
-    ("mm_z", 0, 2),
-    ("square", 2, 3),
+    ("mm_z", 0, 1),
+    ("add_bias", -3, 3),
+    ("silu", 0, 0),
+    ("mm_o", -2, 0),
     ("mix", -1, 1),
-    ("add_bias", -2, 1),
-    ("mm_o", -2, 2),
-    ("silu", 0, 2),
-    ("gate", 0, 0),
-    ("mm_o", -2, 3),
-    ("norm", 1, 3),
-    ("gate", 0, 1),
+    ("scale_x", 1, 0),
+    ("silu", 0, 1),
+    ("mm_o", -2, 1),
+    ("mm_z", 0, 2),
+    ("cast_x", 2, 1),
+    ("norm", 1, 1),
     ("mm_z", 0, 3),
-    ("turn_n", 0, 2),
-    ("add_bias", -2, 2),
-    ("inv_rms", 2, 0),
+    ("scale_x", 1, 1),
+    ("square", 2, 0),
+    ("norm", 1, 2),
+    ("turn_n", 0, 0),
+    ("square", 2, 1),
+    ("add_bias", -2, 0),
+    ("turn_n", 0, 1),
+    ("silu", 0, 2),
+    ("add_bias", -2, 1),
+    ("turn_x", 2, 0),
     ("silu", 0, 3),
-    ("turn_n", 0, 3),
+    ("gate", 0, 0),
+    ("square", 2, 2),
+    ("turn_x", 2, 1),
+    ("gate", 0, 1),
+    ("square", 2, 3),
+    ("turn_n", 0, 2),
     ("load_x", 5, 0),
     ("load_x", 5, 1),
     ("load_h", 5, 0),
@@ -225,14 +226,13 @@ def tile_hstu_pb_t_w4_kernel(
             nc.gpsimd.tensor_tensor(out=rstd[:], in0=ms[:], in1=neg_half[:], op=POW)
 
         def norm(g, j):
-            nc.gpsimd.tensor_scalar(
-                out=n_of(g)[:, j],
-                in0=h_of(g)[:, j, :].rearrange("p (q t) -> p t q", t=PACK),
-                scalar1=made["rstd", g][:, j : j + 1],
-                scalar2=0.0,
-                op0=MULT,
-                op1=ADD,
-            )
+            dst = n_of(g)[:, j]
+            src = h_of(g)[:, j, :].rearrange("p (q t) -> p t q", t=PACK)
+            factor = made["rstd", g][:, j : j + 1]
+            if j in NORM_ON_SCALAR and g > 0:
+                nc.scalar.activation(out=dst, in_=src, func=ACT.Copy, scale=factor)
+            else:
+                nc.gpsimd.tensor_scalar(out=dst, in0=src, scalar1=factor, scalar2=0.0, op0=MULT, op1=ADD)
 
         def turn_n(g, t):
             bank = psum.tile([P, TILES, P], F32, name="nt")

from contextlib import ExitStack

import concourse.mybir as mybir
from concourse.masks import make_identity

TOKENS = 8192
P = 128
K = 512
PACK = 4
TILES = 4
GROUP = TILES * P
EPS = 1.1920928955078125e-07
MIXES = 2
NORM_ON_SCALAR = (3,)

FLOPS = 2 * 2 * TOKENS * K * K

F32 = mybir.dt.float32
BF16 = mybir.dt.bfloat16
I32 = mybir.dt.int32
U32 = mybir.dt.uint32
U8 = mybir.dt.uint8
F8 = mybir.dt.float8_e4m3fn
F8X4 = mybir.dt.float8_e4m3fn_x4
F4X4 = mybir.dt.float4_e2m1fn_x4
MULT = mybir.AluOpType.mult
ADD = mybir.AluOpType.add
POW = mybir.AluOpType.pow
ACT = mybir.ActivationFunctionType

ORDER = (
    ("quant_x", 0, 0),
    ("norm", 0, 3),
    ("turn_n", -1, 3),
    ("quant_uv", -2, 0),
    ("cast_x", 2, 0),
    ("gate", -1, 2),
    ("inv_rms", 1, 0),
    ("mm_o", -3, 2),
    ("norm", 1, 0),
    ("mm_o", -3, 3),
    ("gate", -1, 3),
    ("mm_z", 0, 0),
    ("add_bias", -3, 2),
    ("mix", -1, 0),
    ("mm_z", 0, 1),
    ("add_bias", -3, 3),
    ("silu", 0, 0),
    ("mm_o", -2, 0),
    ("mix", -1, 1),
    ("scale_x", 1, 0),
    ("silu", 0, 1),
    ("mm_o", -2, 1),
    ("mm_z", 0, 2),
    ("cast_x", 2, 1),
    ("norm", 1, 1),
    ("mm_z", 0, 3),
    ("scale_x", 1, 1),
    ("square", 2, 0),
    ("norm", 1, 2),
    ("turn_n", 0, 0),
    ("square", 2, 1),
    ("add_bias", -2, 0),
    ("turn_n", 0, 1),
    ("silu", 0, 2),
    ("add_bias", -2, 1),
    ("turn_x", 2, 0),
    ("silu", 0, 3),
    ("gate", 0, 0),
    ("square", 2, 2),
    ("turn_x", 2, 1),
    ("gate", 0, 1),
    ("square", 2, 3),
    ("turn_n", 0, 2),
    ("load_x", 5, 0),
    ("load_x", 5, 1),
    ("load_h", 5, 0),
)

WEIGHTS_AFTER = ("scale_x", 1, 1)


def tile_hstu_pb_t_w4_kernel(
    tc, x_bytes, x_scale, h_attn, wu_words, wu_scales, bu, g_norm, wf_words, wf_scales, b_out, out
):
    nc = tc.nc
    groups = TOKENS // GROUP
    last = groups - 1

    x_hbm = x_bytes.flatten_outer_dims().rearrange("(g p j) k -> g p (j k)", p=P, j=TILES)
    h_hbm = h_attn.flatten_outer_dims().rearrange("(g p j) k -> g p j k", p=P, j=TILES)
    o_hbm = out.flatten_outer_dims().rearrange("(g p j) k -> g p j k", p=P, j=TILES)

    with ExitStack() as ctx:
        const = ctx.enter_context(tc.tile_pool(name="const", bufs=1))
        two = ctx.enter_context(tc.tile_pool(name="two", bufs=2))
        three = ctx.enter_context(tc.tile_pool(name="three", bufs=3))
        six = ctx.enter_context(tc.tile_pool(name="six", bufs=6))
        psum = ctx.enter_context(tc.psum_pool(name="psum", bufs=2))

        ident = const.tile([P, P], F32, name="ident")
        neg_half = const.tile([P, TILES], F32, name="neg_half")
        warm = const.tile([P, 1], F32, name="warm")
        x_scales = const.tile([P, PACK], F32, name="x_scales")
        bias_raw = const.tile([P, PACK], BF16, name="bias_raw")
        gain_raw = const.tile([P, PACK], BF16, name="gain_raw")
        bias_u = const.tile([P, PACK], F32, name="bias_u")
        gain = const.tile([P, PACK], F32, name="gain")
        bias_out = const.tile([P, K], BF16, name="bias_out")
        wu_raw = const.tile([P, 2 * K], U8, name="wu_raw", align_bytes=64)
        wus_raw = const.tile([P, K], U8, name="wus_raw", align_bytes=64)
        wu = const.tile([P, 2 * K], U8, name="wu", align_bytes=64)
        wus = const.tile([P, K], U8, name="wus", align_bytes=64)
        wf = const.tile([P, 2 * K], U8, name="wf", align_bytes=64)
        wfs = const.tile([P, K], U8, name="wfs", align_bytes=64)

        made = {}

        def tile_of(name, g, pool, shape, dtype):
            if (name, g) not in made:
                made[name, g] = pool.tile(shape, dtype, name=name, align_bytes=64)
            return made[name, g]

        def codes_of_x(g):
            return tile_of("x_codes", g, three, [P, GROUP], U32), tile_of("x_planes", g, three, [P, GROUP], U8)

        def codes_of_uv(g):
            return tile_of("uv_codes", g, two, [P, GROUP], U32), tile_of("uv_planes", g, two, [P, GROUP], U8)

        def x_raw_of(g):
            return tile_of("x_raw", g, six, [P, TILES * K], U8)

        def h_of(g):
            return tile_of("h", g, six, [P, TILES, K], BF16)

        def x_wide_of(g):
            return tile_of("x_wide", g, three, [P, TILES * K], BF16)

        def x_mixed_of(g):
            return tile_of("x_mixed", g, two, [P, GROUP * PACK], BF16)

        def u_of(g):
            return tile_of("u", g, three, [P, PACK, GROUP], F32)

        def n_of(g):
            return tile_of("n", g, two, [P, TILES, PACK, P], F32)

        def uv_of(g):
            return tile_of("uv", g, two, [P, GROUP * PACK], BF16)

        def flat_of(g):
            return tile_of("uv_flat", g, two, [P, PACK, GROUP], BF16)

        def load_x(g, half):
            cols = slice(half * 2 * K, (half + 1) * 2 * K)
            nc.sync.dma_start(out=x_raw_of(g)[:, cols], in_=x_hbm[g][:, cols])

        def load_h(g, whole):
            nc.sync.dma_start(out=h_of(g)[:], in_=h_hbm[g])

        def cast_x(g, half):
            cols = slice(half * 2 * K, (half + 1) * 2 * K)
            nc.scalar.copy(out=x_wide_of(g)[:, cols], in_=x_raw_of(g)[:, cols].bitcast(F8))

        def turn_x(g, half):
            bank = psum.tile([P, 2, 2 * P], F32, name="xt")
            made["xt", g, half] = bank
            words = x_wide_of(g)[:].bitcast(F32)
            for i in range(2):
                first = (half * 2 + i) * (K // 2)
                for u in range(2):
                    nc.tensor.transpose(
                        bank[:, u, i * P : (i + 1) * P], words[:, first + u : first + K // 2 : 2], ident[:]
                    )

        def scale_x(g, half):
            cols = slice(half * 2 * K, (half + 1) * 2 * K)
            nc.vector.tensor_tensor(
                out=x_mixed_of(g)[:, cols].rearrange("p (k u e) -> p k u e", u=2, e=2),
                in0=made["xt", g, half][:]
                .rearrange("p u k -> p (u k)")
                .bitcast(BF16)
                .rearrange("p (u k e) -> p k u e", u=2, e=2),
                in1=x_scales[:].rearrange("p (o u e) -> p o u e", o=1, u=2).to_broadcast([P, 2 * P, 2, 2]),
                op=MULT,
            )

        def quant_x(g, whole):
            codes, planes = codes_of_x(g)
            nc.vector.quantize_mx(out=codes[:].bitcast(F8X4), scales=planes[:], in_=x_mixed_of(g)[:])

        def mm_z(g, t):
            codes, planes = codes_of_x(g)
            bank = psum.tile([P, GROUP], F32, name="z")
            made["z", g, t] = bank
            nc.tensor.matmul_mx(
                out=bank[:],
                lhsT=wu[:, t * 2 * P : (t + 1) * 2 * P].bitcast(F4X4),
                lhsT_scale=wus[:, t * P : (t + 1) * P],
                rhs=codes[:].bitcast(F8X4),
                rhs_scale=planes[:],
                start=True,
                stop=True,
            )

        def silu(g, t):
            nc.scalar.activation(
                out=u_of(g)[:, t, :], in_=made["z", g, t][:], func=ACT.Silu, bias=bias_u[:, t : t + 1]
            )

        def square(g, j):
            junk = two.tile([P, K], BF16, name="junk")
            nc.scalar.activation(
                out=junk[:],
                in_=h_of(g)[:, j, :],
                func=ACT.Square,
                accum_out=tile_of("ssq", g, three, [P, TILES], F32)[:, j : j + 1],
            )

        def inv_rms(g, whole):
            ms = three.tile([P, TILES], F32, name="ms")
            nc.gpsimd.tensor_scalar(
                out=ms[:], in0=made["ssq", g][:], scalar1=1.0 / K, scalar2=EPS, op0=MULT, op1=ADD
            )
            rstd = tile_of("rstd", g, three, [P, TILES], F32)
            nc.gpsimd.tensor_tensor(out=rstd[:], in0=ms[:], in1=neg_half[:], op=POW)

        def norm(g, j):
            dst = n_of(g)[:, j]
            src = h_of(g)[:, j, :].rearrange("p (q t) -> p t q", t=PACK)
            factor = made["rstd", g][:, j : j + 1]
            if j in NORM_ON_SCALAR and g > 0:
                nc.scalar.activation(out=dst, in_=src, func=ACT.Copy, scale=factor)
            else:
                nc.gpsimd.tensor_scalar(out=dst, in0=src, scalar1=factor, scalar2=0.0, op0=MULT, op1=ADD)

        def turn_n(g, t):
            bank = psum.tile([P, TILES, P], F32, name="nt")
            made["nt", g, t] = bank
            for j in range(TILES):
                nc.tensor.transpose(bank[:, j, :], n_of(g)[:, j, t, :], ident[:])

        def gate(g, t):
            nc.vector.scalar_tensor_tensor(
                out=flat_of(g)[:, t, :],
                in0=made["nt", g, t][:].rearrange("p j q -> p (j q)"),
                scalar=gain[:, t : t + 1],
                in1=u_of(g)[:, t, :],
                op0=MULT,
                op1=MULT,
            )

        def mix(g, part):
            width = GROUP // MIXES
            cols = slice(part * width, (part + 1) * width)
            dst = uv_of(g)[:].rearrange("p (k t) -> p k t", t=PACK)[:, cols]
            src = flat_of(g)[:, :, cols].rearrange("p t k -> p k t")
            if g == last:
                nc.vector.tensor_copy(out=dst, in_=src)
            else:
                nc.gpsimd.tensor_scalar(out=dst, in0=src, scalar1=1.0, scalar2=0.0, op0=MULT, op1=ADD)

        def quant_uv(g, whole):
            codes, planes = codes_of_uv(g)
            nc.vector.quantize_mx(out=codes[:].bitcast(F8X4), scales=planes[:], in_=uv_of(g)[:])

        def mm_o(g, j):
            codes, planes = codes_of_uv(g)
            bank = psum.tile([P, K], F32, name="o")
            made["o", g, j] = bank
            cols = slice(j * P, (j + 1) * P)
            nc.tensor.matmul_mx(
                out=bank[:],
                lhsT=codes[:, cols].bitcast(F8X4),
                lhsT_scale=planes[:, cols],
                rhs=wf[:].bitcast(F4X4),
                rhs_scale=wfs[:],
                start=True,
                stop=True,
            )

        def add_bias(g, j):
            res = tile_of("res", g, three, [P, TILES, K], F32)
            nc.vector.tensor_tensor(out=res[:, j, :], in0=made["o", g, j][:], in1=bias_out[:], op=ADD)
            if g == last:
                nc.sync.dma_start(out=o_hbm[g][:, j], in_=res[:, j])
            elif j == TILES - 1:
                nc.sync.dma_start(out=o_hbm[g], in_=res[:])

        steps = {
            "load_x": load_x,
            "load_h": load_h,
            "cast_x": cast_x,
            "turn_x": turn_x,
            "scale_x": scale_x,
            "quant_x": quant_x,
            "mm_z": mm_z,
            "silu": silu,
            "square": square,
            "inv_rms": inv_rms,
            "norm": norm,
            "turn_n": turn_n,
            "gate": gate,
            "mix": mix,
            "quant_uv": quant_uv,
            "mm_o": mm_o,
            "add_bias": add_bias,
        }
        issued = set()

        def issue(step, g, part):
            if 0 <= g < groups and (step, g, part) not in issued:
                issued.add((step, g, part))
                steps[step](g, part)

        with tc.manual_schedule():
            nc.vector.memset(warm[:], 0.0)
            nc.scalar.activation(out=warm[:], in_=warm[:], func=ACT.Silu)
            nc.vector.memset(wus_raw[:].bitcast(I32), 0)
            nc.vector.memset(wfs[:].bitcast(I32), 0)
            nc.vector.memset(neg_half[:], -0.5)
            make_identity(nc, ident[:])

            issue("load_x", 0, 0)
            issue("load_x", 0, 1)
            nc.scalar.dma_start(out=x_scales[:], in_=x_scale.rearrange("a b (p t) -> p (a b t)", t=PACK))
            nc.scalar.dma_start(out=bias_raw[:], in_=bu.rearrange("(p t) -> p t", t=PACK))
            nc.scalar.dma_start(out=gain_raw[:], in_=g_norm.rearrange("(p t) -> p t", t=PACK))
            issue("load_h", 0, 0)
            nc.sync.dma_start(out=wu_raw[:], in_=wu_words[0])
            for q in range(4):
                nc.sync.dma_start(
                    out=wus_raw[32 * q : 32 * q + 4, :].bitcast(I32),
                    in_=wu_scales[0, 4 * q : 4 * q + 4, :].bitcast(I32),
                )
            issue("load_x", 1, 0)
            issue("load_x", 1, 1)
            issue("load_h", 1, 0)
            nc.sync.dma_start(out=wf[:], in_=wf_words[0])
            for q in range(4):
                nc.sync.dma_start(
                    out=wfs[32 * q : 32 * q + 4, :].bitcast(I32),
                    in_=wf_scales[0, 4 * q : 4 * q + 4, :].bitcast(I32),
                )
            nc.sync.dma_start(out=bias_out[:], in_=b_out.partition_broadcast(P))
            for g in range(2, 6):
                issue("load_x", g, 0)
                issue("load_x", g, 1)
                issue("load_h", g, 0)


            issue("cast_x", 0, 0)
            issue("cast_x", 0, 1)
            issue("turn_x", 0, 0)
            issue("turn_x", 0, 1)
            for s in range(-6, groups + 4):
                for step, ahead, part in ORDER:
                    issue(step, s + ahead, part)
                    if (step, ahead, part) == WEIGHTS_AFTER and s + ahead == 0:
                        nc.vector.tensor_copy(
                            out=wu[:].rearrange("p (t m b) -> p t m b", t=PACK, b=2),
                            in_=wu_raw[:].rearrange("p (m t b) -> p t m b", t=PACK, b=2),
                        )
                        nc.vector.tensor_copy(
                            out=wus[:].rearrange("p (t m) -> p t m", t=PACK),
                            in_=wus_raw[:].rearrange("p (m t) -> p t m", t=PACK),
                        )
                        nc.vector.tensor_copy(out=bias_u[:], in_=bias_raw[:])
                        nc.vector.tensor_copy(out=gain[:], in_=gain_raw[:])
